import numpy as np
import ml_dtypes


def mxq(x, axis, fmt="e4m3"):
    dtype, down = {"e4m3": (ml_dtypes.float8_e4m3fn, 7), "e5m2": (ml_dtypes.float8_e5m2, 14)}[fmt]
    v = np.moveaxis(np.asarray(x, np.float32).astype(ml_dtypes.bfloat16).astype(np.float64), axis, -1)
    blocks = v.reshape(v.shape[:-1] + (-1, 32))
    amax = np.abs(blocks).max(-1, keepdims=True)
    byte = np.maximum(np.where(amax > 0, np.frexp(amax)[1] - 1 + 127, 0) - down, 1)
    scale = np.exp2(byte - 127.0)
    codes = (blocks / scale).astype(np.float32).astype(dtype).astype(np.float64)
    return np.moveaxis((codes * scale).reshape(v.shape), -1, axis)


WIDE = False


def mx_kscale(k):
    if not WIDE:
        return np.ones(k)
    levels = np.array([10, -10, 5, -5, 0])
    if k % 512:
        return np.exp2(np.random.permutation(np.resize(levels, k // 32))).repeat(32)
    a = np.empty((k // 512, 16))
    for p in range(k // 512):
        a[p, :8] = np.random.permutation(np.resize(levels, 8))
        for g in range(8):
            far = levels[np.abs(levels - a[p, g]) >= 10]
            a[p, g + 8] = far[np.random.randint(len(far))]
    return np.exp2(a.ravel()).repeat(32)


BF16 = ml_dtypes.bfloat16


def bf(x):
    return np.asarray(x, np.float32).astype(BF16)


def f64(x):
    return np.asarray(x).astype(np.float64)


B, S, D, H, HD = 4, 1024, 512, 4, 96
DPA = HD // 6


def build_rope_freqs():
    return 1.0 / (10000.0 ** (np.arange(DPA) / DPA))


def apply_rope_3d(t, coords, freqs):
    theta = (coords[..., None] * freqs).reshape(*coords.shape[:-1], -1)[:, None]
    cos, sin = np.cos(theta), np.sin(theta)
    tp = t.reshape(*t.shape[:-1], t.shape[-1] // 2, 2)
    t1, t2 = tp[..., 0], tp[..., 1]
    out = np.stack([t1 * cos - t2 * sin, t1 * sin + t2 * cos], axis=-1)
    return out.reshape(t.shape)


def setup_inputs():
    s = mx_kscale(D)
    return {'x': bf(np.random.standard_normal((B, S, D)) * s),
            'coords': bf(np.random.standard_normal((B, S, 3))),
            'W_qkv': bf(np.random.standard_normal((3 * H * HD, D)) / np.sqrt(D) / s)}


def reference(x, coords, W_qkv):
    freqs = build_rope_freqs()
    c = f64(coords)
    qkv = mxq(f64(x), 2, 'e4m3') @ mxq(f64(W_qkv), 1, 'e4m3').T
    qkv = qkv.reshape(B, S, 3, H, HD)
    q, k, v = (qkv[:, :, i].transpose(0, 2, 1, 3) for i in range(3))
    return apply_rope_3d(q, c, freqs), apply_rope_3d(k, c, freqs), v

@@ -1,0 +1,219 @@
+import math
+from contextlib import ExitStack
+
+import concourse.mybir as mybir
+from concourse.masks import make_identity
+
+F32 = mybir.dt.float32
+BF16 = mybir.dt.bfloat16
+U32 = mybir.dt.uint32
+U8 = mybir.dt.uint8
+FP8X4 = mybir.dt.float8_e4m3fn_x4
+ALU = mybir.AluOpType
+ACT = mybir.ActivationFunctionType
+
+P = 128
+PACK = 4
+B, S, D, H, HD = 4, 1024, 512, 4, 96
+PAIRS = HD // 2
+AXES = 3
+FREQS = PAIRS // AXES
+COLS = H * HD
+TILES_PER_BATCH = S // P
+TILES = B * TILES_PER_BATCH
+W_TILES = 3 * COLS // P
+WORDS = D // 2
+GROUP = 4
+ADD_TILES = 2
+ROUND_MAGIC = 1.5 * 2.0**23
+
+FLOPS = 2 * B * S * D * 3 * COLS
+
+
+def transpose_and_quantise(nc, copy, flip_pool, stage, identity, row_tiles, codes, scales):
+    count = len(row_tiles)
+    grouped = stage.tile([P, GROUP * P * PACK], BF16, align_bytes=64)
+    grouped_words = grouped[:].bitcast(F32).rearrange("p (i r u) -> p i r u", r=P, u=2)
+    for first in range(0, count, 2):
+        pair = row_tiles[first : first + 2]
+        flipped = flip_pool.tile([P, 2, 2, P], F32)
+        for i, rows in enumerate(pair):
+            for u in range(2):
+                nc.tensor.transpose(flipped[:, i, u, :], rows[:, u:WORDS:2], identity[:])
+        copy(
+            out=grouped_words[:, first : first + len(pair)],
+            in_=flipped[:, 0 : len(pair)].rearrange("p i u r -> p i r u"),
+        )
+    nc.vector.quantize_mx(
+        out=codes.bitcast(FP8X4), scales=scales, in_=grouped[:, 0 : count * P * PACK]
+    )
+
+
+def tile_ropeattention_pa_t_kernel(tc, x, coords, W_qkv, out_0, out_1, out_2):
+    nc = tc.nc
+    with ExitStack() as ctx:
+        keep = ctx.enter_context(tc.tile_pool(name="keep", bufs=1))
+        stage = ctx.enter_context(tc.tile_pool(name="stage", bufs=2))
+        work = ctx.enter_context(tc.tile_pool(name="work", bufs=3))
+        flip_pool = ctx.enter_context(tc.psum_pool(name="flip", bufs=2))
+        acc_pool = ctx.enter_context(tc.psum_pool(name="acc", bufs=2))
+
+        coords_sb = keep.tile([P, B, TILES_PER_BATCH, AXES], BF16)
+        nc.scalar.dma_start(
+            out=coords_sb[:], in_=coords.rearrange("b (p t) a -> p b t a", t=TILES_PER_BATCH)
+        )
+        w_sb = keep.tile([P, W_TILES, D], BF16)
+        w_rows = W_qkv.rearrange("(n p) k -> p n k", p=P)
+        x_sb = keep.tile([P, B, TILES_PER_BATCH, D], BF16)
+        x_rows = x.rearrange("b (p t) k -> b p t k", t=TILES_PER_BATCH)
+        nc.sync.dma_start(out=w_sb[:, 0:GROUP], in_=w_rows[:, 0:GROUP])
+        nc.sync.dma_start(out=x_sb[:, 0, 0:GROUP], in_=x_rows[0, :, 0:GROUP])
+        nc.sync.dma_start(out=w_sb[:, GROUP:W_TILES], in_=w_rows[:, GROUP:W_TILES])
+        nc.sync.dma_start(out=x_sb[:, 0, GROUP:], in_=x_rows[0, :, GROUP:])
+        for b in range(1, B):
+            nc.sync.dma_start(out=x_sb[:, b], in_=x_rows[b])
+
+        identity = keep.tile([P, P], F32)
+        make_identity(nc, identity[:])
+
+        turn_freqs = keep.tile([P, FREQS], F32)
+        nc.vector.memset(turn_freqs[:, 0:1], 1.0)
+        warm = keep.tile([P, 2], F32)
+        nc.gpsimd.memset(warm[:, 0:1], 0.0)
+        nc.scalar.activation(out=warm[:, 1:2], in_=warm[:, 0:1], func=ACT.Sin)
+        nc.vector.tensor_scalar(
+            out=turn_freqs[:, 0:1], in0=turn_freqs[:, 0:1],
+            scalar1=1.0 / (2.0 * math.pi), scalar2=None, op0=ALU.mult,
+        )
+        filled = 1
+        while filled < FREQS:
+            nc.vector.tensor_scalar(
+                out=turn_freqs[:, filled : 2 * filled], in0=turn_freqs[:, 0:filled],
+                scalar1=10000.0 ** (-filled / FREQS), scalar2=None, op0=ALU.mult,
+            )
+            filled *= 2
+
+        table = keep.tile([P, TILES, 3, PAIRS], F32)
+        ANGLES = TILES_PER_BATCH * AXES
+
+        def fill_table(b):
+            turns = stage.tile([P, ANGLES, FREQS], F32)
+            part = stage.tile([P, ANGLES, FREQS], F32)
+            nc.vector.tensor_tensor(
+                out=turns[:],
+                in0=coords_sb[:, b].rearrange("p t a -> p (t a)").unsqueeze(2)
+                .to_broadcast([P, ANGLES, FREQS]),
+                in1=turn_freqs[:].unsqueeze(1).to_broadcast([P, ANGLES, FREQS]),
+                op=ALU.mult,
+            )
+            nc.vector.tensor_scalar(
+                out=part[:], in0=turns[:], scalar1=ROUND_MAGIC, scalar2=ROUND_MAGIC,
+                op0=ALU.add, op1=ALU.subtract,
+            )
+            nc.vector.tensor_tensor(out=part[:], in0=turns[:], in1=part[:], op=ALU.subtract)
+            by_tile = part[:].rearrange("p (t a) j -> p t (a j)", a=AXES)
+            rows = table[:, b * TILES_PER_BATCH : (b + 1) * TILES_PER_BATCH]
+            nc.scalar.activation(out=rows[:, :, 2, :], in_=by_tile, func=ACT.Sin, scale=2.0 * math.pi)
+            nc.scalar.activation(out=rows[:, :, 0, :], in_=by_tile, func=ACT.Sin, scale=-2.0 * math.pi)
+            half_sin = turns
+            nc.scalar.activation(out=half_sin[:], in_=part[:], func=ACT.Sin, scale=math.pi)
+            nc.scalar.activation(out=half_sin[:], in_=half_sin[:], func=ACT.Square)
+            nc.vector.tensor_scalar(
+                out=rows[:, :, 1, :], in0=half_sin[:].rearrange("p (t a) j -> p t (a j)", a=AXES),
+                scalar1=-2.0, scalar2=1.0, op0=ALU.mult, op1=ALU.add,
+            )
+
+        x_codes = keep.tile([P, TILES * P], U32, align_bytes=64)
+        x_scales = keep.tile([P, TILES * P], U8, align_bytes=64)
+        x_words = x_sb[:].bitcast(F32)
+
+        def quantise_x(g):
+            b, first = divmod(g * GROUP, TILES_PER_BATCH)
+            cols = slice(g * GROUP * P, (g + 1) * GROUP * P)
+            transpose_and_quantise(
+                nc, nc.scalar.copy, flip_pool, stage, identity,
+                [x_words[:, b, t, :] for t in range(first, first + GROUP)],
+                x_codes[:, cols], x_scales[:, cols],
+            )
+
+        w_codes = keep.tile([P, 3 * COLS], U32, align_bytes=64)
+        w_scales = keep.tile([P, 3 * COLS], U8, align_bytes=64)
+        w_words = w_sb[:].bitcast(F32)
+
+        def quantise_w(first):
+            count = min(GROUP, W_TILES - first)
+            cols = slice(first * P, (first + count) * P)
+            transpose_and_quantise(
+                nc, nc.vector.tensor_copy, flip_pool, stage, identity,
+                [w_words[:, n, :] for n in range(first, first + count)],
+                w_codes[:, cols], w_scales[:, cols],
+            )
+
+        fill_table(0)
+        quantise_w(0)
+        quantise_x(0)
+        quantise_w(GROUP)
+        quantise_w(2 * GROUP)
+
+        GROUPS = TILES // GROUP
+        for g in range(GROUPS):
+            b, first = divmod(g * GROUP, TILES_PER_BATCH)
+            rotated = work.tile([P, 2 * H, GROUP, HD], F32)
+            plain_v = work.tile([P, H, GROUP, HD], F32)
+            for j0 in range(0, GROUP, ADD_TILES):
+                from_even = work.tile([P, 2 * H, ADD_TILES, 2, PAIRS], F32)
+                from_odd = work.tile([P, 2 * H, ADD_TILES, 2, PAIRS], F32)
+                for jj in range(ADD_TILES):
+                    i = g * GROUP + j0 + jj
+                    tokens = slice(i * P, (i + 1) * P)
+                    acc = []
+                    for c in range(3):
+                        bank = acc_pool.tile([P, COLS], F32, name="bank%d" % c)
+                        for lo, width in ((0, 256), (256, 128)):
+                            nc.tensor.matmul_mx(
+                                out=bank[:, lo : lo + width],
+                                lhsT=x_codes[:, tokens].bitcast(FP8X4),
+                                lhsT_scale=x_scales[:, tokens],
+                                rhs=w_codes[:, c * COLS + lo : c * COLS + lo + width].bitcast(FP8X4),
+                                rhs_scale=w_scales[:, c * COLS + lo : c * COLS + lo + width],
+                                start=True,
+                                stop=True,
+                            )
+                        acc.append(bank)
+                    for c in range(2):
+                        halves = acc[c][:].rearrange("p (h n e) -> p h e n", h=H, e=2)
+                        heads = slice(c * H, (c + 1) * H)
+                        nc.vector.tensor_tensor(
+                            out=from_even[:, heads, jj],
+                            in0=halves[:, :, 0:1, :].to_broadcast([P, H, 2, PAIRS]),
+                            in1=table[:, i, 1:3, :].unsqueeze(1).to_broadcast([P, H, 2, PAIRS]),
+                            op=ALU.mult,
+                        )
+                        nc.vector.tensor_tensor(
+                            out=from_odd[:, heads, jj],
+                            in0=halves[:, :, 1:2, :].to_broadcast([P, H, 2, PAIRS]),
+                            in1=table[:, i, 0:2, :].unsqueeze(1).to_broadcast([P, H, 2, PAIRS]),
+                            op=ALU.mult,
+                        )
+                    nc.scalar.copy(
+                        out=plain_v[:, :, j0 + jj, :],
+                        in_=acc[2][:].rearrange("p (h d) -> p h d", h=H),
+                    )
+                nc.gpsimd.tensor_tensor(
+                    out=rotated[:, :, j0 : j0 + ADD_TILES, :].rearrange("p m j (n e) -> p m j n e", e=2),
+                    in0=from_even[:].rearrange("p m j e n -> p m j n e"),
+                    in1=from_odd[:].rearrange("p m j e n -> p m j n e"),
+                    op=ALU.add,
+                )
+                if j0 == 0 and g + 1 < GROUPS:
+                    quantise_x(g + 1)
+                if j0 == 0 and first == 0 and b + 1 < B:
+                    fill_table(b + 1)
+            rows = slice(first, first + GROUP)
+            views = [
+                o[b].rearrange("h (p t) d -> p h t d", t=TILES_PER_BATCH)[:, :, rows, :]
+                for o in (out_0, out_1, out_2)
+            ]
+            nc.sync.dma_start(out=views[2], in_=plain_v[:])
+            nc.sync.dma_start(out=views[0], in_=rotated[:, 0:H])
+            nc.sync.dma_start(out=views[1], in_=rotated[:, H : 2 * H])

@@ -21,32 +21,13 @@ FREQS = PAIRS // AXES
 COLS = H * HD
 TILES_PER_BATCH = S // P
 TILES = B * TILES_PER_BATCH
-W_TILES = 3 * COLS // P
+QK_BLOCKS = 2 * COLS // (2 * P)
+V_BLOCKS = COLS // P
 WORDS = D // 2
 GROUP = 4
-ADD_TILES = 2
 ROUND_MAGIC = 1.5 * 2.0**23
 
 FLOPS = 2 * B * S * D * 3 * COLS
-
-
-def transpose_and_quantise(nc, copy, flip_pool, stage, identity, row_tiles, codes, scales):
-    count = len(row_tiles)
-    grouped = stage.tile([P, GROUP * P * PACK], BF16, align_bytes=64)
-    grouped_words = grouped[:].bitcast(F32).rearrange("p (i r u) -> p i r u", r=P, u=2)
-    for first in range(0, count, 2):
-        pair = row_tiles[first : first + 2]
-        flipped = flip_pool.tile([P, 2, 2, P], F32)
-        for i, rows in enumerate(pair):
-            for u in range(2):
-                nc.tensor.transpose(flipped[:, i, u, :], rows[:, u:WORDS:2], identity[:])
-        copy(
-            out=grouped_words[:, first : first + len(pair)],
-            in_=flipped[:, 0 : len(pair)].rearrange("p i u r -> p i r u"),
-        )
-    nc.vector.quantize_mx(
-        out=codes.bitcast(FP8X4), scales=scales, in_=grouped[:, 0 : count * P * PACK]
-    )
 
 
 def tile_ropeattention_pa_t_kernel(tc, x, coords, W_qkv, out_0, out_1, out_2):
@@ -54,21 +35,26 @@ def tile_ropeattention_pa_t_kernel(tc, x, coords, W_qkv, out_0, out_1, out_2):
     with ExitStack() as ctx:
         keep = ctx.enter_context(tc.tile_pool(name="keep", bufs=1))
         stage = ctx.enter_context(tc.tile_pool(name="stage", bufs=2))
-        work = ctx.enter_context(tc.tile_pool(name="work", bufs=3))
-        flip_pool = ctx.enter_context(tc.psum_pool(name="flip", bufs=2))
-        acc_pool = ctx.enter_context(tc.psum_pool(name="acc", bufs=2))
+        work = ctx.enter_context(tc.tile_pool(name="work", bufs=4))
+        flip_pool = ctx.enter_context(tc.psum_pool(name="flips", bufs=2))
+        acc_pool = ctx.enter_context(tc.psum_pool(name="accs", bufs=4))
+        v_pool = ctx.enter_context(tc.psum_pool(name="vs", bufs=2))
+        ctx.enter_context(tc.manual_schedule())
 
         coords_sb = keep.tile([P, B, TILES_PER_BATCH, AXES], BF16)
         nc.scalar.dma_start(
             out=coords_sb[:], in_=coords.rearrange("b (p t) a -> p b t a", t=TILES_PER_BATCH)
         )
-        w_sb = keep.tile([P, W_TILES, D], BF16)
-        w_rows = W_qkv.rearrange("(n p) k -> p n k", p=P)
+        wqk_sb = keep.tile([P, QK_BLOCKS, 2, D], BF16)
+        wqk_rows = W_qkv[0 : 2 * COLS].rearrange("(n p e) k -> n p e k", p=P, e=2)
+        wv_sb = keep.tile([P, V_BLOCKS, D], BF16)
+        wv_rows = W_qkv[2 * COLS : 3 * COLS].rearrange("(n p) k -> p n k", p=P)
         x_sb = keep.tile([P, B, TILES_PER_BATCH, D], BF16)
         x_rows = x.rearrange("b (p t) k -> b p t k", t=TILES_PER_BATCH)
-        nc.sync.dma_start(out=w_sb[:, 0:GROUP], in_=w_rows[:, 0:GROUP])
+        for n in range(QK_BLOCKS):
+            nc.sync.dma_start(out=wqk_sb[:, n], in_=wqk_rows[n])
         nc.sync.dma_start(out=x_sb[:, 0, 0:GROUP], in_=x_rows[0, :, 0:GROUP])
-        nc.sync.dma_start(out=w_sb[:, GROUP:W_TILES], in_=w_rows[:, GROUP:W_TILES])
+        nc.sync.dma_start(out=wv_sb[:], in_=wv_rows)
         nc.sync.dma_start(out=x_sb[:, 0, GROUP:], in_=x_rows[0, :, GROUP:])
         for b in range(1, B):
             nc.sync.dma_start(out=x_sb[:, b], in_=x_rows[b])
@@ -76,13 +62,11 @@ def tile_ropeattention_pa_t_kernel(tc, x, coords, W_qkv, out_0, out_1, out_2):
         identity = keep.tile([P, P], F32)
         make_identity(nc, identity[:])
 
+        ones = keep.tile([P, 1], F32)
+        nc.vector.memset(ones[:], 1.0)
         turn_freqs = keep.tile([P, FREQS], F32)
-        nc.vector.memset(turn_freqs[:, 0:1], 1.0)
-        warm = keep.tile([P, 2], F32)
-        nc.gpsimd.memset(warm[:, 0:1], 0.0)
-        nc.scalar.activation(out=warm[:, 1:2], in_=warm[:, 0:1], func=ACT.Sin)
         nc.vector.tensor_scalar(
-            out=turn_freqs[:, 0:1], in0=turn_freqs[:, 0:1],
+            out=turn_freqs[:, 0:1], in0=ones[:],
             scalar1=1.0 / (2.0 * math.pi), scalar2=None, op0=ALU.mult,
         )
         filled = 1
@@ -92,13 +76,22 @@ def tile_ropeattention_pa_t_kernel(tc, x, coords, W_qkv, out_0, out_1, out_2):
                 scalar1=10000.0 ** (-filled / FREQS), scalar2=None, op0=ALU.mult,
             )
             filled *= 2
+        biases = keep.tile([P, 4], F32)
+        for w, value in enumerate((0.0, 0.25, -0.25, -0.5)):
+            nc.vector.tensor_scalar(
+                out=biases[:, w : w + 1], in0=ones[:],
+                scalar1=value * math.pi, scalar2=None, op0=ALU.mult,
+            )
+        warm = keep.tile([P, 1], F32)
+        nc.scalar.activation(out=warm[:], in_=ones[:], func=ACT.Sin)
 
         table = keep.tile([P, TILES, 3, PAIRS], F32)
         ANGLES = TILES_PER_BATCH * AXES
+        fraction = keep.tile([P, B, ANGLES, FREQS], F32)
 
-        def fill_table(b):
+        def reduce_angles(b):
             turns = stage.tile([P, ANGLES, FREQS], F32)
-            part = stage.tile([P, ANGLES, FREQS], F32)
+            whole = stage.tile([P, ANGLES, FREQS], F32)
             nc.vector.tensor_tensor(
                 out=turns[:],
                 in0=coords_sb[:, b].rearrange("p t a -> p (t a)").unsqueeze(2)
@@ -107,113 +100,208 @@ def tile_ropeattention_pa_t_kernel(tc, x, coords, W_qkv, out_0, out_1, out_2):
                 op=ALU.mult,
             )
             nc.vector.tensor_scalar(
-                out=part[:], in0=turns[:], scalar1=ROUND_MAGIC, scalar2=ROUND_MAGIC,
+                out=whole[:], in0=turns[:], scalar1=ROUND_MAGIC, scalar2=ROUND_MAGIC,
                 op0=ALU.add, op1=ALU.subtract,
             )
-            nc.vector.tensor_tensor(out=part[:], in0=turns[:], in1=part[:], op=ALU.subtract)
-            by_tile = part[:].rearrange("p (t a) j -> p t (a j)", a=AXES)
-            rows = table[:, b * TILES_PER_BATCH : (b + 1) * TILES_PER_BATCH]
-            nc.scalar.activation(out=rows[:, :, 2, :], in_=by_tile, func=ACT.Sin, scale=2.0 * math.pi)
-            nc.scalar.activation(out=rows[:, :, 0, :], in_=by_tile, func=ACT.Sin, scale=-2.0 * math.pi)
-            half_sin = turns
-            nc.scalar.activation(out=half_sin[:], in_=part[:], func=ACT.Sin, scale=math.pi)
-            nc.scalar.activation(out=half_sin[:], in_=half_sin[:], func=ACT.Square)
-            nc.vector.tensor_scalar(
-                out=rows[:, :, 1, :], in0=half_sin[:].rearrange("p (t a) j -> p t (a j)", a=AXES),
-                scalar1=-2.0, scalar2=1.0, op0=ALU.mult, op1=ALU.add,
-            )
+            nc.vector.tensor_tensor(out=fraction[:, b], in0=turns[:], in1=whole[:], op=ALU.subtract)
 
-        x_codes = keep.tile([P, TILES * P], U32, align_bytes=64)
-        x_scales = keep.tile([P, TILES * P], U8, align_bytes=64)
-        x_words = x_sb[:].bitcast(F32)
+        def fill_table_steps(b):
+            folded = stage.tile([P, TILES_PER_BATCH, 3, PAIRS], F32)
 
-        def quantise_x(g):
-            b, first = divmod(g * GROUP, TILES_PER_BATCH)
-            cols = slice(g * GROUP * P, (g + 1) * GROUP * P)
-            transpose_and_quantise(
-                nc, nc.scalar.copy, flip_pool, stage, identity,
-                [x_words[:, b, t, :] for t in range(first, first + GROUP)],
-                x_codes[:, cols], x_scales[:, cols],
+            def fold(w):
+                nc.scalar.activation(
+                    out=folded[:, :, w, :],
+                    in_=fraction[:, b].rearrange("p (t a) j -> p t (a j)", a=AXES),
+                    func=ACT.Abs, scale=2.0 * math.pi, bias=biases[:, w : w + 1],
+                )
+
+            def sines():
+                nc.scalar.activation(
+                    out=table[:, b * TILES_PER_BATCH : (b + 1) * TILES_PER_BATCH],
+                    in_=folded[:], func=ACT.Sin, bias=biases[:, 3:4],
+                )
+
+            return [lambda: fold(0), lambda: fold(1), lambda: fold(2), sines]
+
+        def flip(bank, slot, rows):
+            for u in range(2):
+                nc.tensor.transpose(bank[:, slot, u, :], rows[:, u:WORDS:2], identity[:])
+
+        def regroup(copy, grouped, bank, slots):
+            copy(
+                out=grouped.bitcast(F32).rearrange("p (i r u) -> p i r u", r=P, u=2),
+                in_=bank[:, 0:slots].rearrange("p i u r -> p i r u"),
             )
 
         w_codes = keep.tile([P, 3 * COLS], U32, align_bytes=64)
         w_scales = keep.tile([P, 3 * COLS], U8, align_bytes=64)
-        w_words = w_sb[:].bitcast(F32)
+        x_codes = keep.tile([P, TILES * P], U32, align_bytes=64)
+        x_scales = keep.tile([P, TILES * P], U8, align_bytes=64)
+        wqk_words = wqk_sb[:].bitcast(F32)
+        wv_words = wv_sb[:].bitcast(F32)
+        x_words = x_sb[:].bitcast(F32)
 
-        def quantise_w(first):
-            count = min(GROUP, W_TILES - first)
-            cols = slice(first * P, (first + count) * P)
-            transpose_and_quantise(
-                nc, nc.vector.tensor_copy, flip_pool, stage, identity,
-                [w_words[:, n, :] for n in range(first, first + count)],
-                w_codes[:, cols], w_scales[:, cols],
+        def quantise(codes, scales, grouped):
+            nc.vector.quantize_mx(out=codes.bitcast(FP8X4), scales=scales, in_=grouped)
+
+        def w_flips(tiles):
+            bank = acc_pool.tile([P, 2, 2, P], F32, name="bank")
+            for slot, rows in enumerate(tiles):
+                flip(bank, slot, rows)
+            return bank
+
+        def w_regroup(copy, bank, count):
+            grouped = stage.tile([P, 2 * P * PACK], BF16, align_bytes=64, name="w_grouped", bufs=3)
+            regroup(copy, grouped[:, 0 : count * P * PACK], bank, count)
+            return grouped
+
+        def w_quantise(grouped, columns):
+            for slot, first in enumerate(columns):
+                cols = slice(first, first + P)
+                quantise(
+                    w_codes[:, cols], w_scales[:, cols],
+                    grouped[:, slot * P * PACK : (slot + 1) * P * PACK],
+                )
+
+        def x_flips(g):
+            b, first = divmod(g * GROUP, TILES_PER_BATCH)
+            banks = []
+            for half in range(2):
+                bank = flip_pool.tile([P, 2, 2, P], F32, name="flip")
+                for slot in range(2):
+                    flip(bank, slot, x_words[:, b, first + 2 * half + slot, :])
+                banks.append(bank)
+            return banks
+
+        def x_regroup(banks):
+            grouped = stage.tile([P, GROUP * P * PACK], BF16, align_bytes=64, name="x_grouped")
+            for half, bank in enumerate(banks):
+                regroup(
+                    nc.scalar.copy,
+                    grouped[:, 2 * half * P * PACK : 2 * (half + 1) * P * PACK], bank, 2,
+                )
+            return grouped
+
+        def x_quantise(g, grouped):
+            cols = slice(g * GROUP * P, (g + 1) * GROUP * P)
+            quantise(x_codes[:, cols], x_scales[:, cols], grouped[:])
+
+        def passes(bank, i, col0s):
+            tokens = slice(i * P, (i + 1) * P)
+            for lo, width in ((0, 256), (256, 128)):
+                for n, col0 in enumerate(col0s):
+                    cols = slice(col0 + lo, col0 + lo + width)
+                    nc.tensor.matmul_mx(
+                        out=bank[:, lo : lo + width],
+                        lhsT=x_codes[:, tokens].bitcast(FP8X4),
+                        lhsT_scale=x_scales[:, tokens],
+                        rhs=w_codes[:, cols].bitcast(FP8X4),
+                        rhs_scale=w_scales[:, cols],
+                        start=(n == 0),
+                        stop=(n == len(col0s) - 1),
+                    )
+
+        def multiply(i):
+            banks = []
+            for col0s in ((0,), (COLS,), (0, COLS)):
+                bank = acc_pool.tile([P, COLS], F32, name="bank")
+                passes(bank, i, col0s)
+                banks.append(bank)
+            v_bank = v_pool.tile([P, COLS], F32, name="v_bank")
+            passes(v_bank, i, (2 * COLS,))
+            return banks, v_bank
+
+        def products(i, banks):
+            shared = work.tile([P, 2 * H, PAIRS], F32)
+            own = work.tile([P, 2 * H, 2, PAIRS], F32)
+            root2 = math.sqrt(2.0)
+            for bank, w, factor, out in (
+                (banks[0], 1, root2, own[:, :, 1, :]),
+                (banks[1], 2, root2, own[:, :, 0, :]),
+                (banks[2], 0, -1.0, shared[:]),
+            ):
+                nc.vector.scalar_tensor_tensor(
+                    out=out,
+                    in0=bank[:].rearrange("p (m n) -> p m n", m=2 * H),
+                    scalar=factor,
+                    in1=table[:, i, w, :].unsqueeze(1).to_broadcast([P, 2 * H, PAIRS]),
+                    op0=ALU.mult,
+                    op1=ALU.mult,
+                )
+            return shared, own
+
+        def add(engine, rotated, j, shared, own):
+            engine.tensor_tensor(
+                out=rotated[:, :, j, :].rearrange("p m (n e) -> p m n e", e=2),
+                in0=shared[:].unsqueeze(3).to_broadcast([P, 2 * H, PAIRS, 2]),
+                in1=own[:].rearrange("p m e n -> p m n e"),
+                op=ALU.add,
             )
 
-        fill_table(0)
-        quantise_w(0)
-        quantise_x(0)
-        quantise_w(GROUP)
-        quantise_w(2 * GROUP)
+        for b in range(B):
+            if b < 1:
+                reduce_angles(b)
+        for step in fill_table_steps(0):
+            step()
+        w_banks = [w_flips([wqk_words[:, n, e, :] for e in range(2)]) for n in range(QK_BLOCKS)]
+        x_banks = x_flips(0)
+        for n in range(QK_BLOCKS):
+            grouped = w_regroup(nc.vector.tensor_copy, w_banks[n], 2)
+            w_quantise(grouped, (n * P, COLS + n * P))
+        x_grouped = x_regroup(x_banks)
+        x_quantise(0, x_grouped)
+        for first, count in ((0, 2), (2, 1)):
+            bank = w_flips([wv_words[:, first + s, :] for s in range(count)])
+            grouped = w_regroup(nc.scalar.copy, bank, count)
+            w_quantise(grouped, [2 * COLS + (first + s) * P for s in range(count)])
 
         GROUPS = TILES // GROUP
+
+        def store_v(b, first, plain_v):
+            rows = slice(first, first + GROUP)
+            view = out_2[b].rearrange("h (p t) d -> p h t d", t=TILES_PER_BATCH)
+            nc.sync.dma_start(out=view[:, :, rows, :], in_=plain_v[:])
+
+        def store_qk(b, first, rotated):
+            rows = slice(first, first + GROUP)
+            for c, o in enumerate((out_0, out_1)):
+                view = o[b].rearrange("h (p t) d -> p h t d", t=TILES_PER_BATCH)
+                nc.sync.dma_start(out=view[:, :, rows, :], in_=rotated[:, c * H : (c + 1) * H])
+
+        def finish(b, first, rotated, j, shared, own):
+            add(nc.vector, rotated, j, shared, own)
+            store_qk(b, first, rotated)
+
+        steps = []
+        late = None
         for g in range(GROUPS):
             b, first = divmod(g * GROUP, TILES_PER_BATCH)
             rotated = work.tile([P, 2 * H, GROUP, HD], F32)
             plain_v = work.tile([P, H, GROUP, HD], F32)
-            for j0 in range(0, GROUP, ADD_TILES):
-                from_even = work.tile([P, 2 * H, ADD_TILES, 2, PAIRS], F32)
-                from_odd = work.tile([P, 2 * H, ADD_TILES, 2, PAIRS], F32)
-                for jj in range(ADD_TILES):
-                    i = g * GROUP + j0 + jj
-                    tokens = slice(i * P, (i + 1) * P)
-                    acc = []
-                    for c in range(3):
-                        bank = acc_pool.tile([P, COLS], F32, name="bank%d" % c)
-                        for lo, width in ((0, 256), (256, 128)):
-                            nc.tensor.matmul_mx(
-                                out=bank[:, lo : lo + width],
-                                lhsT=x_codes[:, tokens].bitcast(FP8X4),
-                                lhsT_scale=x_scales[:, tokens],
-                                rhs=w_codes[:, c * COLS + lo : c * COLS + lo + width].bitcast(FP8X4),
-                                rhs_scale=w_scales[:, c * COLS + lo : c * COLS + lo + width],
-                                start=True,
-                                stop=True,
-                            )
-                        acc.append(bank)
-                    for c in range(2):
-                        halves = acc[c][:].rearrange("p (h n e) -> p h e n", h=H, e=2)
-                        heads = slice(c * H, (c + 1) * H)
-                        nc.vector.tensor_tensor(
-                            out=from_even[:, heads, jj],
-                            in0=halves[:, :, 0:1, :].to_broadcast([P, H, 2, PAIRS]),
-                            in1=table[:, i, 1:3, :].unsqueeze(1).to_broadcast([P, H, 2, PAIRS]),
-                            op=ALU.mult,
-                        )
-                        nc.vector.tensor_tensor(
-                            out=from_odd[:, heads, jj],
-                            in0=halves[:, :, 1:2, :].to_broadcast([P, H, 2, PAIRS]),
-                            in1=table[:, i, 0:2, :].unsqueeze(1).to_broadcast([P, H, 2, PAIRS]),
-                            op=ALU.mult,
-                        )
-                    nc.scalar.copy(
-                        out=plain_v[:, :, j0 + jj, :],
-                        in_=acc[2][:].rearrange("p (h d) -> p h d", h=H),
-                    )
-                nc.gpsimd.tensor_tensor(
-                    out=rotated[:, :, j0 : j0 + ADD_TILES, :].rearrange("p m j (n e) -> p m j n e", e=2),
-                    in0=from_even[:].rearrange("p m j e n -> p m j n e"),
-                    in1=from_odd[:].rearrange("p m j e n -> p m j n e"),
-                    op=ALU.add,
+            for j in range(GROUP):
+                i = g * GROUP + j
+                banks, v_bank = multiply(i)
+                if j == 1 and g + 1 < GROUPS:
+                    x_banks = x_flips(g + 1)
+                shared, own = products(i, banks)
+                nc.scalar.copy(
+                    out=plain_v[:, :, j, :], in_=v_bank[:].rearrange("p (h d) -> p h d", h=H)
                 )
-                if j0 == 0 and g + 1 < GROUPS:
-                    quantise_x(g + 1)
-                if j0 == 0 and first == 0 and b + 1 < B:
-                    fill_table(b + 1)
-            rows = slice(first, first + GROUP)
-            views = [
-                o[b].rearrange("h (p t) d -> p h t d", t=TILES_PER_BATCH)[:, :, rows, :]
-                for o in (out_0, out_1, out_2)
-            ]
-            nc.sync.dma_start(out=views[2], in_=plain_v[:])
-            nc.sync.dma_start(out=views[0], in_=rotated[:, 0:H])
-            nc.sync.dma_start(out=views[1], in_=rotated[:, H : 2 * H])
+                if j == 1 and g + 1 < GROUPS:
+                    x_grouped = x_regroup(x_banks)
+                if j == 2 and g + 1 < GROUPS:
+                    x_quantise(g + 1, x_grouped)
+                if late is not None:
+                    finish(*late)
+                    late = None
+                if j < GROUP - 1:
+                    add(nc.gpsimd, rotated, j, shared, own)
+                else:
+                    late = (b, first, rotated, j, shared, own)
+                if first == 0 and j == 0 and b + 1 < B:
+                    reduce_angles(b + 1)
+                    steps = fill_table_steps(b + 1)
+                if (first == 0 and j >= 2 or first > 0) and steps:
+                    steps.pop(0)()
+            store_v(b, first, plain_v)
+        finish(*late)

@@ -1,5 +1,6 @@
 import math
 from contextlib import ExitStack
+from functools import partial
 
 import concourse.mybir as mybir
 from concourse.masks import make_identity
@@ -25,6 +26,8 @@ QK_BLOCKS = 2 * COLS // (2 * P)
 V_BLOCKS = COLS // P
 WORDS = D // 2
 GROUP = 4
+LATE = 3
+DUO = 2
 ROUND_MAGIC = 1.5 * 2.0**23
 
 FLOPS = 2 * B * S * D * 3 * COLS
@@ -53,7 +56,8 @@ def tile_ropeattention_pa_t_kernel(tc, x, coords, W_qkv, out_0, out_1, out_2):
         x_rows = x.rearrange("b (p t) k -> b p t k", t=TILES_PER_BATCH)
         for n in range(QK_BLOCKS):
             nc.sync.dma_start(out=wqk_sb[:, n], in_=wqk_rows[n])
-        nc.sync.dma_start(out=x_sb[:, 0, 0:GROUP], in_=x_rows[0, :, 0:GROUP])
+        for t in range(0, GROUP, DUO):
+            nc.sync.dma_start(out=x_sb[:, 0, t : t + DUO], in_=x_rows[0, :, t : t + DUO])
         nc.sync.dma_start(out=wv_sb[:], in_=wv_rows)
         nc.sync.dma_start(out=x_sb[:, 0, GROUP:], in_=x_rows[0, :, GROUP:])
         for b in range(1, B):
@@ -89,39 +93,40 @@ def tile_ropeattention_pa_t_kernel(tc, x, coords, W_qkv, out_0, out_1, out_2):
         ANGLES = TILES_PER_BATCH * AXES
         fraction = keep.tile([P, B, ANGLES, FREQS], F32)
 
-        def reduce_angles(b):
+        def reduce_angles(engine, b):
             turns = stage.tile([P, ANGLES, FREQS], F32)
             whole = stage.tile([P, ANGLES, FREQS], F32)
-            nc.vector.tensor_tensor(
+            engine.tensor_tensor(
                 out=turns[:],
                 in0=coords_sb[:, b].rearrange("p t a -> p (t a)").unsqueeze(2)
                 .to_broadcast([P, ANGLES, FREQS]),
                 in1=turn_freqs[:].unsqueeze(1).to_broadcast([P, ANGLES, FREQS]),
                 op=ALU.mult,
             )
-            nc.vector.tensor_scalar(
+            engine.tensor_scalar(
                 out=whole[:], in0=turns[:], scalar1=ROUND_MAGIC, scalar2=ROUND_MAGIC,
                 op0=ALU.add, op1=ALU.subtract,
             )
-            nc.vector.tensor_tensor(out=fraction[:, b], in0=turns[:], in1=whole[:], op=ALU.subtract)
+            engine.tensor_tensor(out=fraction[:, b], in0=turns[:], in1=whole[:], op=ALU.subtract)
 
-        def fill_table_steps(b):
+        def fill_table_steps(b, first, count):
             folded = stage.tile([P, TILES_PER_BATCH, 3, PAIRS], F32)
+            angles = fraction[:, b].rearrange("p (t a) j -> p t (a j)", a=AXES)
 
             def fold(w):
                 nc.scalar.activation(
-                    out=folded[:, :, w, :],
-                    in_=fraction[:, b].rearrange("p (t a) j -> p t (a j)", a=AXES),
+                    out=folded[:, 0:count, w, :], in_=angles[:, first : first + count],
                     func=ACT.Abs, scale=2.0 * math.pi, bias=biases[:, w : w + 1],
                 )
 
             def sines():
+                i = b * TILES_PER_BATCH + first
                 nc.scalar.activation(
-                    out=table[:, b * TILES_PER_BATCH : (b + 1) * TILES_PER_BATCH],
-                    in_=folded[:], func=ACT.Sin, bias=biases[:, 3:4],
+                    out=table[:, i : i + count], in_=folded[:, 0:count],
+                    func=ACT.Sin, bias=biases[:, 3:4],
                 )
 
-            return [lambda: fold(0), lambda: fold(1), lambda: fold(2), sines]
+            return [partial(fold, 0), partial(fold, 1), partial(fold, 2), sines]
 
         def flip(bank, slot, rows):
             for u in range(2):
@@ -144,16 +149,10 @@ def tile_ropeattention_pa_t_kernel(tc, x, coords, W_qkv, out_0, out_1, out_2):
         def quantise(codes, scales, grouped):
             nc.vector.quantize_mx(out=codes.bitcast(FP8X4), scales=scales, in_=grouped)
 
-        def w_flips(tiles):
-            bank = acc_pool.tile([P, 2, 2, P], F32, name="bank")
+        def w_flips(bank, tiles):
             for slot, rows in enumerate(tiles):
                 flip(bank, slot, rows)
             return bank
-
-        def w_regroup(copy, bank, count):
-            grouped = stage.tile([P, 2 * P * PACK], BF16, align_bytes=64, name="w_grouped", bufs=3)
-            regroup(copy, grouped[:, 0 : count * P * PACK], bank, count)
-            return grouped
 
         def w_quantise(grouped, columns):
             for slot, first in enumerate(columns):
@@ -163,28 +162,20 @@ def tile_ropeattention_pa_t_kernel(tc, x, coords, W_qkv, out_0, out_1, out_2):
                     grouped[:, slot * P * PACK : (slot + 1) * P * PACK],
                 )
 
-        def x_flips(g):
-            b, first = divmod(g * GROUP, TILES_PER_BATCH)
-            banks = []
-            for half in range(2):
-                bank = flip_pool.tile([P, 2, 2, P], F32, name="flip")
-                for slot in range(2):
-                    flip(bank, slot, x_words[:, b, first + 2 * half + slot, :])
-                banks.append(bank)
-            return banks
+        def x_flips(first):
+            b, t = divmod(first, TILES_PER_BATCH)
+            bank = flip_pool.tile([P, DUO, 2, P], F32, name="flip")
+            for slot in range(DUO):
+                flip(bank, slot, x_words[:, b, t + slot, :])
+            return bank
 
-        def x_regroup(banks):
-            grouped = stage.tile([P, GROUP * P * PACK], BF16, align_bytes=64, name="x_grouped")
-            for half, bank in enumerate(banks):
-                regroup(
-                    nc.scalar.copy,
-                    grouped[:, 2 * half * P * PACK : 2 * (half + 1) * P * PACK], bank, 2,
-                )
-            return grouped
+        def x_regroup(grouped, duo, bank):
+            columns = slice(duo * DUO * P * PACK, (duo + 1) * DUO * P * PACK)
+            regroup(nc.scalar.copy, grouped[:, columns], bank, DUO)
 
-        def x_quantise(g, grouped):
-            cols = slice(g * GROUP * P, (g + 1) * GROUP * P)
-            quantise(x_codes[:, cols], x_scales[:, cols], grouped[:])
+        def x_quantise(first, count, grouped):
+            cols = slice(first * P, (first + count) * P)
+            quantise(x_codes[:, cols], x_scales[:, cols], grouped)
 
         def passes(bank, i, col0s):
             tokens = slice(i * P, (i + 1) * P)
@@ -201,15 +192,18 @@ def tile_ropeattention_pa_t_kernel(tc, x, coords, W_qkv, out_0, out_1, out_2):
                         stop=(n == len(col0s) - 1),
                     )
 
-        def multiply(i):
+        def multiply_qk(i):
             banks = []
             for col0s in ((0,), (COLS,), (0, COLS)):
                 bank = acc_pool.tile([P, COLS], F32, name="bank")
                 passes(bank, i, col0s)
                 banks.append(bank)
+            return banks
+
+        def multiply_v(i):
             v_bank = v_pool.tile([P, COLS], F32, name="v_bank")
             passes(v_bank, i, (2 * COLS,))
-            return banks, v_bank
+            return v_bank
 
         def products(i, banks):
             shared = work.tile([P, 2 * H, PAIRS], F32)
@@ -238,70 +232,97 @@ def tile_ropeattention_pa_t_kernel(tc, x, coords, W_qkv, out_0, out_1, out_2):
                 op=ALU.add,
             )
 
-        for b in range(B):
-            if b < 1:
-                reduce_angles(b)
-        for step in fill_table_steps(0):
+        def store(o, b, first, count, tile):
+            view = o[b].rearrange("h (p t) d -> p h t d", t=TILES_PER_BATCH)
+            nc.sync.dma_start(out=view[:, :, first : first + count, :], in_=tile)
+
+        reduce_angles(nc.vector, 0)
+        for b in range(1, B):
+            reduce_angles(nc.gpsimd, b)
+        steps = fill_table_steps(0, 0, GROUP)
+        for step in steps[0:3]:
             step()
-        w_banks = [w_flips([wqk_words[:, n, e, :] for e in range(2)]) for n in range(QK_BLOCKS)]
-        x_banks = x_flips(0)
+        grouped_w = [
+            stage.tile([P, 2 * P * PACK], BF16, align_bytes=64, name="w_grouped%d" % n)
+            for n in range(QK_BLOCKS)
+        ]
+        w_banks = []
         for n in range(QK_BLOCKS):
-            grouped = w_regroup(nc.vector.tensor_copy, w_banks[n], 2)
-            w_quantise(grouped, (n * P, COLS + n * P))
-        x_grouped = x_regroup(x_banks)
-        x_quantise(0, x_grouped)
+            bank = acc_pool.tile([P, 2, 2, P], F32, name="bank")
+            w_banks.append(w_flips(bank, [wqk_words[:, n, e, :] for e in range(2)]))
+        x_banks = [x_flips(first) for first in range(0, GROUP, DUO)]
+        regroup(nc.vector.tensor_copy, grouped_w[0][:], w_banks[0], 2)
+        regroup(nc.scalar.copy, grouped_w[1][:], w_banks[1], 2)
+        steps[3]()
+        w_quantise(grouped_w[0], (0, COLS))
+        w_quantise(grouped_w[1], (P, COLS + P))
+        regroup(nc.vector.tensor_copy, grouped_w[2][:], w_banks[2], 2)
+        w_quantise(grouped_w[2], (2 * P, COLS + 2 * P))
+        x_grouped = stage.tile([P, GROUP * P * PACK], BF16, align_bytes=64, name="x_grouped")
+        for duo, bank in enumerate(x_banks):
+            x_regroup(x_grouped, duo, bank)
+        half = DUO * P * PACK
+        x_quantise(0, DUO, x_grouped[:, 0:half])
+        qk_banks = multiply_qk(0)
+        wv_banks = []
         for first, count in ((0, 2), (2, 1)):
-            bank = w_flips([wv_words[:, first + s, :] for s in range(count)])
-            grouped = w_regroup(nc.scalar.copy, bank, count)
-            w_quantise(grouped, [2 * COLS + (first + s) * P for s in range(count)])
+            bank = v_pool.tile([P, 2, 2, P], F32, name="v_bank")
+            w_flips(bank, [wv_words[:, first + s, :] for s in range(count)])
+            wv_banks.append(bank)
+        grouped_v = [
+            stage.tile([P, 2 * P * PACK], BF16, align_bytes=64, name="v_grouped%d" % n)
+            for n in range(2)
+        ]
+        regroup(nc.scalar.copy, grouped_v[0][:], wv_banks[0], 2)
+        regroup(nc.scalar.copy, grouped_v[1][:, 0 : P * PACK], wv_banks[1], 1)
 
-        GROUPS = TILES // GROUP
-
-        def store_v(b, first, plain_v):
-            rows = slice(first, first + GROUP)
-            view = out_2[b].rearrange("h (p t) d -> p h t d", t=TILES_PER_BATCH)
-            nc.sync.dma_start(out=view[:, :, rows, :], in_=plain_v[:])
-
-        def store_qk(b, first, rotated):
-            rows = slice(first, first + GROUP)
-            for c, o in enumerate((out_0, out_1)):
-                view = o[b].rearrange("h (p t) d -> p h t d", t=TILES_PER_BATCH)
-                nc.sync.dma_start(out=view[:, :, rows, :], in_=rotated[:, c * H : (c + 1) * H])
-
-        def finish(b, first, rotated, j, shared, own):
-            add(nc.vector, rotated, j, shared, own)
-            store_qk(b, first, rotated)
-
-        steps = []
-        late = None
-        for g in range(GROUPS):
-            b, first = divmod(g * GROUP, TILES_PER_BATCH)
-            rotated = work.tile([P, 2 * H, GROUP, HD], F32)
-            plain_v = work.tile([P, H, GROUP, HD], F32)
-            for j in range(GROUP):
-                i = g * GROUP + j
-                banks, v_bank = multiply(i)
-                if j == 1 and g + 1 < GROUPS:
-                    x_banks = x_flips(g + 1)
-                shared, own = products(i, banks)
-                nc.scalar.copy(
-                    out=plain_v[:, :, j, :], in_=v_bank[:].rearrange("p (h d) -> p h d", h=H)
-                )
-                if j == 1 and g + 1 < GROUPS:
-                    x_grouped = x_regroup(x_banks)
-                if j == 2 and g + 1 < GROUPS:
-                    x_quantise(g + 1, x_grouped)
-                if late is not None:
-                    finish(*late)
-                    late = None
-                if j < GROUP - 1:
-                    add(nc.gpsimd, rotated, j, shared, own)
-                else:
-                    late = (b, first, rotated, j, shared, own)
-                if first == 0 and j == 0 and b + 1 < B:
-                    reduce_angles(b + 1)
-                    steps = fill_table_steps(b + 1)
-                if (first == 0 and j >= 2 or first > 0) and steps:
-                    steps.pop(0)()
-            store_v(b, first, plain_v)
-        finish(*late)
+        for step in fill_table_steps(0, GROUP, GROUP):
+            step()
+        late = []
+        for i in range(TILES):
+            b, t = divmod(i, TILES_PER_BATCH)
+            j = i % GROUP
+            if j == 0:
+                rotated = work.tile([P, 2 * H, GROUP, HD], F32)
+                plain_v = work.tile([P, H, GROUP, HD], F32)
+            shared, own = products(i, qk_banks)
+            if i == 0:
+                x_quantise(DUO, DUO, x_grouped[:, half : 2 * half])
+                w_quantise(grouped_v[0], (2 * COLS, 2 * COLS + P))
+                w_quantise(grouped_v[1], (2 * COLS + 2 * P,))
+            if j == 2 and i + GROUP < TILES:
+                x_quantise(i - j + GROUP, GROUP, x_grouped[:])
+            if i + 1 < TILES:
+                qk_banks = multiply_qk(i + 1)
+            v_bank = multiply_v(i)
+            if j == 0 and i + GROUP < TILES:
+                x_banks = [x_flips(i + GROUP + duo) for duo in range(0, GROUP, DUO)]
+            nc.scalar.copy(
+                out=plain_v[:, :, j, :], in_=v_bank[:].rearrange("p (h d) -> p h d", h=H)
+            )
+            if j == 0 and i + GROUP < TILES:
+                x_grouped = stage.tile([P, GROUP * P * PACK], BF16, align_bytes=64, name="x_grouped")
+            if j < 2 and i + GROUP < TILES:
+                x_regroup(x_grouped, j, x_banks[j])
+            if i < 4 * (B - 1):
+                if i % 4 == 0:
+                    steps = fill_table_steps(i // 4 + 1, 0, TILES_PER_BATCH)
+                steps[i % 4]()
+            if i < TILES - LATE:
+                add(nc.gpsimd, rotated, j, shared, own)
+            else:
+                late.append((rotated, j, shared, own))
+            if j == GROUP - 1:
+                store(out_2, b, t - j, GROUP, plain_v[:])
+                for c, o in enumerate((out_0, out_1)):
+                    if i < TILES - 1:
+                        store(o, b, t - j, GROUP, rotated[:, c * H : (c + 1) * H])
+        for n, args in enumerate(late):
+            add(nc.vector, *args)
+            if n % DUO == 0:
+                first = GROUP - LATE + n - 1
+                for c, o in enumerate((out_0, out_1)):
+                    store(
+                        o, B - 1, TILES_PER_BATCH - GROUP + first, DUO,
+                        rotated[:, c * H : (c + 1) * H, first : first + DUO],
+                    )

@@ -26,7 +26,6 @@ QK_BLOCKS = 2 * COLS // (2 * P)
 V_BLOCKS = COLS // P
 WORDS = D // 2
 GROUP = 4
-LATE = 3
 DUO = 2
 ROUND_MAGIC = 1.5 * 2.0**23
 
@@ -236,6 +235,14 @@ def tile_ropeattention_pa_t_kernel(tc, x, coords, W_qkv, out_0, out_1, out_2):
             view = o[b].rearrange("h (p t) d -> p h t d", t=TILES_PER_BATCH)
             nc.sync.dma_start(out=view[:, :, first : first + count, :], in_=tile)
 
+        def finish(b, t, rotated, j, shared, own):
+            add(nc.vector, rotated, j, shared, own)
+            count = DUO if b == B - 1 and t >= TILES_PER_BATCH - GROUP else GROUP
+            if (j + 1) % count == 0:
+                for c, o in enumerate((out_0, out_1)):
+                    heads = slice(c * H, (c + 1) * H)
+                    store(o, b, t + 1 - count, count, rotated[:, heads, j + 1 - count : j + 1])
+
         reduce_angles(nc.vector, 0)
         for b in range(1, B):
             reduce_angles(nc.gpsimd, b)
@@ -308,21 +315,9 @@ def tile_ropeattention_pa_t_kernel(tc, x, coords, W_qkv, out_0, out_1, out_2):
                 if i % 4 == 0:
                     steps = fill_table_steps(i // 4 + 1, 0, TILES_PER_BATCH)
                 steps[i % 4]()
-            if i < TILES - LATE:
-                add(nc.gpsimd, rotated, j, shared, own)
-            else:
-                late.append((rotated, j, shared, own))
+            late.append((b, t, rotated, j, shared, own))
+            if len(late) > 1:
+                finish(*late.pop(0))
             if j == GROUP - 1:
                 store(out_2, b, t - j, GROUP, plain_v[:])
-                for c, o in enumerate((out_0, out_1)):
-                    if i < TILES - 1:
-                        store(o, b, t - j, GROUP, rotated[:, c * H : (c + 1) * H])
-        for n, args in enumerate(late):
-            add(nc.vector, *args)
-            if n % DUO == 0:
-                first = GROUP - LATE + n - 1
-                for c, o in enumerate((out_0, out_1)):
-                    store(
-                        o, B - 1, TILES_PER_BATCH - GROUP + first, DUO,
-                        rotated[:, c * H : (c + 1) * H, first : first + DUO],
-                    )
+        finish(*late.pop(0))

@@ -38,6 +38,7 @@ def tile_ropeattention_pa_t_kernel(tc, x, coords, W_qkv, out_0, out_1, out_2):
         keep = ctx.enter_context(tc.tile_pool(name="keep", bufs=1))
         stage = ctx.enter_context(tc.tile_pool(name="stage", bufs=2))
         work = ctx.enter_context(tc.tile_pool(name="work", bufs=4))
+        outs = ctx.enter_context(tc.tile_pool(name="outs", bufs=3))
         flip_pool = ctx.enter_context(tc.psum_pool(name="flips", bufs=2))
         acc_pool = ctx.enter_context(tc.psum_pool(name="accs", bufs=4))
         v_pool = ctx.enter_context(tc.psum_pool(name="vs", bufs=2))
@@ -92,21 +93,23 @@ def tile_ropeattention_pa_t_kernel(tc, x, coords, W_qkv, out_0, out_1, out_2):
         ANGLES = TILES_PER_BATCH * AXES
         fraction = keep.tile([P, B, ANGLES, FREQS], F32)
 
-        def reduce_angles(engine, b):
-            turns = stage.tile([P, ANGLES, FREQS], F32)
-            whole = stage.tile([P, ANGLES, FREQS], F32)
-            engine.tensor_tensor(
+        def reduce_angles(first, count):
+            shape = [P, count * ANGLES, FREQS]
+            turns = keep.tile(shape, F32, name="turns%d" % first)
+            whole = keep.tile(shape, F32, name="whole%d" % first)
+            nc.vector.tensor_tensor(
                 out=turns[:],
-                in0=coords_sb[:, b].rearrange("p t a -> p (t a)").unsqueeze(2)
-                .to_broadcast([P, ANGLES, FREQS]),
-                in1=turn_freqs[:].unsqueeze(1).to_broadcast([P, ANGLES, FREQS]),
+                in0=coords_sb[:, first : first + count].rearrange("p b t a -> p (b t a)").unsqueeze(2)
+                .to_broadcast(shape),
+                in1=turn_freqs[:].unsqueeze(1).to_broadcast(shape),
                 op=ALU.mult,
             )
-            engine.tensor_scalar(
+            nc.vector.tensor_scalar(
                 out=whole[:], in0=turns[:], scalar1=ROUND_MAGIC, scalar2=ROUND_MAGIC,
                 op0=ALU.add, op1=ALU.subtract,
             )
-            engine.tensor_tensor(out=fraction[:, b], in0=turns[:], in1=whole[:], op=ALU.subtract)
+            nc.vector.tensor_tensor(
+                out=fraction[:, first : first + count].rearrange("p b q j -> p (b q) j"), in0=turns[:], in1=whole[:], op=ALU.subtract)
 
         def fill_table_steps(b, first, count):
             folded = stage.tile([P, TILES_PER_BATCH, 3, PAIRS], F32)
@@ -204,15 +207,10 @@ def tile_ropeattention_pa_t_kernel(tc, x, coords, W_qkv, out_0, out_1, out_2):
             passes(v_bank, i, (2 * COLS,))
             return v_bank
 
-        def products(i, banks):
-            shared = work.tile([P, 2 * H, PAIRS], F32)
-            own = work.tile([P, 2 * H, 2, PAIRS], F32)
+        def product_steps(i, banks, slot, shared, own):
             root2 = math.sqrt(2.0)
-            for bank, w, factor, out in (
-                (banks[0], 1, root2, own[:, :, 1, :]),
-                (banks[1], 2, root2, own[:, :, 0, :]),
-                (banks[2], 0, -1.0, shared[:]),
-            ):
+
+            def product(bank, w, factor, out):
                 nc.vector.scalar_tensor_tensor(
                     out=out,
                     in0=bank[:].rearrange("p (m n) -> p m n", m=2 * H),
@@ -221,103 +219,126 @@ def tile_ropeattention_pa_t_kernel(tc, x, coords, W_qkv, out_0, out_1, out_2):
                     op0=ALU.mult,
                     op1=ALU.mult,
                 )
-            return shared, own
 
-        def add(engine, rotated, j, shared, own):
+            return [
+                partial(product, banks[0], 1, root2, own[:, :, slot, 1, :]),
+                partial(product, banks[1], 2, root2, own[:, :, slot, 0, :]),
+                partial(product, banks[2], 0, -1.0, shared[:, :, slot, :]),
+            ]
+
+        def add(engine, rotated, j, shared, own, heads):
+            count = heads.stop - heads.start
             engine.tensor_tensor(
-                out=rotated[:, :, j, :].rearrange("p m (n e) -> p m n e", e=2),
-                in0=shared[:].unsqueeze(3).to_broadcast([P, 2 * H, PAIRS, 2]),
-                in1=own[:].rearrange("p m e n -> p m n e"),
+                out=rotated[:, heads, j : j + DUO, :].rearrange("p m j (n e) -> p m j n e", e=2),
+                in0=shared[:, heads].unsqueeze(4).to_broadcast([P, count, DUO, PAIRS, 2]),
+                in1=own[:, heads].rearrange("p m j e n -> p m j n e"),
                 op=ALU.add,
             )
 
-        def store(o, b, first, count, tile):
+        def store(o, b, t, count, tile):
             view = o[b].rearrange("h (p t) d -> p h t d", t=TILES_PER_BATCH)
-            nc.sync.dma_start(out=view[:, :, first : first + count, :], in_=tile)
+            nc.sync.dma_start(out=view[:, :, t : t + count, :], in_=tile)
 
-        def finish(b, t, rotated, j, shared, own):
-            add(nc.vector, rotated, j, shared, own)
-            count = DUO if b == B - 1 and t >= TILES_PER_BATCH - GROUP else GROUP
-            if (j + 1) % count == 0:
-                for c, o in enumerate((out_0, out_1)):
-                    heads = slice(c * H, (c + 1) * H)
-                    store(o, b, t + 1 - count, count, rotated[:, heads, j + 1 - count : j + 1])
+        q_heads, k_heads, all_heads = slice(0, H), slice(H, 2 * H), slice(0, 2 * H)
 
-        reduce_angles(nc.vector, 0)
-        for b in range(1, B):
-            reduce_angles(nc.gpsimd, b)
-        steps = fill_table_steps(0, 0, GROUP)
-        for step in steps[0:3]:
-            step()
-        grouped_w = [
-            stage.tile([P, 2 * P * PACK], BF16, align_bytes=64, name="w_grouped%d" % n)
+        reduce_angles(0, 1)
+        reduce_angles(1, 1)
+        w_grouped = [
+            keep.tile([P, 2 * P * PACK], BF16, align_bytes=64, name="w_grouped%d" % n)
             for n in range(QK_BLOCKS)
         ]
         w_banks = []
         for n in range(QK_BLOCKS):
             bank = acc_pool.tile([P, 2, 2, P], F32, name="bank")
-            w_banks.append(w_flips(bank, [wqk_words[:, n, e, :] for e in range(2)]))
+            w_flips(bank, [wqk_words[:, n, e, :] for e in range(2)])
+            w_banks.append(bank)
         x_banks = [x_flips(first) for first in range(0, GROUP, DUO)]
-        regroup(nc.vector.tensor_copy, grouped_w[0][:], w_banks[0], 2)
-        regroup(nc.scalar.copy, grouped_w[1][:], w_banks[1], 2)
+        steps = fill_table_steps(0, 0, GROUP)
+        for step in steps[0:3]:
+            step()
+        regroup(nc.scalar.copy, w_grouped[0][:], w_banks[0], 2)
+        regroup(nc.vector.tensor_copy, w_grouped[1][:], w_banks[1], 2)
         steps[3]()
-        w_quantise(grouped_w[0], (0, COLS))
-        w_quantise(grouped_w[1], (P, COLS + P))
-        regroup(nc.vector.tensor_copy, grouped_w[2][:], w_banks[2], 2)
-        w_quantise(grouped_w[2], (2 * P, COLS + 2 * P))
+        w_quantise(w_grouped[0], (0, COLS))
+        regroup(nc.vector.tensor_copy, w_grouped[2][:], w_banks[2], 2)
+        w_quantise(w_grouped[1], (P, COLS + P))
+        w_quantise(w_grouped[2], (2 * P, COLS + 2 * P))
         x_grouped = stage.tile([P, GROUP * P * PACK], BF16, align_bytes=64, name="x_grouped")
         for duo, bank in enumerate(x_banks):
             x_regroup(x_grouped, duo, bank)
         half = DUO * P * PACK
         x_quantise(0, DUO, x_grouped[:, 0:half])
         qk_banks = multiply_qk(0)
-        wv_banks = []
-        for first, count in ((0, 2), (2, 1)):
-            bank = v_pool.tile([P, 2, 2, P], F32, name="v_bank")
-            w_flips(bank, [wv_words[:, first + s, :] for s in range(count)])
-            wv_banks.append(bank)
-        grouped_v = [
-            stage.tile([P, 2 * P * PACK], BF16, align_bytes=64, name="v_grouped%d" % n)
+        v_grouped = [
+            keep.tile([P, 2 * P * PACK], BF16, align_bytes=64, name="v_grouped%d" % n)
             for n in range(2)
         ]
-        regroup(nc.scalar.copy, grouped_v[0][:], wv_banks[0], 2)
-        regroup(nc.scalar.copy, grouped_v[1][:, 0 : P * PACK], wv_banks[1], 1)
-
+        for n, (first, count) in enumerate(((0, 2), (2, 1))):
+            bank = v_pool.tile([P, 2, 2, P], F32, name="v_bank")
+            w_flips(bank, [wv_words[:, first + s, :] for s in range(count)])
+            regroup(nc.scalar.copy, v_grouped[n][:, 0 : count * P * PACK], bank, count)
         for step in fill_table_steps(0, GROUP, GROUP):
             step()
-        late = []
-        for i in range(TILES):
-            b, t = divmod(i, TILES_PER_BATCH)
-            j = i % GROUP
-            if j == 0:
-                rotated = work.tile([P, 2 * H, GROUP, HD], F32)
-                plain_v = work.tile([P, H, GROUP, HD], F32)
-            shared, own = products(i, qk_banks)
-            if i == 0:
-                x_quantise(DUO, DUO, x_grouped[:, half : 2 * half])
-                w_quantise(grouped_v[0], (2 * COLS, 2 * COLS + P))
-                w_quantise(grouped_v[1], (2 * COLS + 2 * P,))
-            if j == 2 and i + GROUP < TILES:
-                x_quantise(i - j + GROUP, GROUP, x_grouped[:])
-            if i + 1 < TILES:
-                qk_banks = multiply_qk(i + 1)
-            v_bank = multiply_v(i)
-            if j == 0 and i + GROUP < TILES:
-                x_banks = [x_flips(i + GROUP + duo) for duo in range(0, GROUP, DUO)]
-            nc.scalar.copy(
-                out=plain_v[:, :, j, :], in_=v_bank[:].rearrange("p (h d) -> p h d", h=H)
-            )
-            if j == 0 and i + GROUP < TILES:
-                x_grouped = stage.tile([P, GROUP * P * PACK], BF16, align_bytes=64, name="x_grouped")
-            if j < 2 and i + GROUP < TILES:
-                x_regroup(x_grouped, j, x_banks[j])
-            if i < 4 * (B - 1):
-                if i % 4 == 0:
-                    steps = fill_table_steps(i // 4 + 1, 0, TILES_PER_BATCH)
-                steps[i % 4]()
-            late.append((b, t, rotated, j, shared, own))
-            if len(late) > 1:
-                finish(*late.pop(0))
-            if j == GROUP - 1:
-                store(out_2, b, t - j, GROUP, plain_v[:])
-        finish(*late.pop(0))
+
+        def operand_flips(g):
+            return [x_flips(g * GROUP + duo) for duo in range(0, GROUP, DUO)]
+
+        def operand_regroup(banks):
+            grouped = stage.tile([P, GROUP * P * PACK], BF16, align_bytes=64, name="x_grouped")
+            for duo, bank in enumerate(banks):
+                x_regroup(grouped, duo, bank)
+            return grouped
+
+        GROUPS = TILES // GROUP
+        for g in range(GROUPS):
+            b, t = divmod(g * GROUP, TILES_PER_BATCH)
+            rotated = outs.tile([P, 2 * H, GROUP, HD], F32)
+            plain_v = outs.tile([P, H, GROUP, HD], F32)
+            for j in range(GROUP):
+                i = g * GROUP + j
+                slot = j % DUO
+                if slot == 0:
+                    shared = work.tile([P, 2 * H, DUO, PAIRS], F32)
+                    own = work.tile([P, 2 * H, DUO, 2, PAIRS], F32)
+                if j == 0:
+                    early = (shared, own)
+                steps = product_steps(i, qk_banks, slot, shared, own)
+                for step in steps[0:2]:
+                    step()
+                if j == GROUP - 1:
+                    add(nc.vector, rotated, 0, early[0], early[1], all_heads)
+                    if g + 2 < GROUPS:
+                        x_quantise((g + 2) * GROUP, GROUP, x_grouped[:])
+                steps[2]()
+                if g == 0 and j == 0:
+                    x_quantise(DUO, DUO, x_grouped[:, half : 2 * half])
+                    w_quantise(v_grouped[0], (2 * COLS, 2 * COLS + P))
+                    w_quantise(v_grouped[1], (2 * COLS + 2 * P,))
+                if i + 1 < TILES:
+                    qk_banks = multiply_qk(i + 1)
+                v_bank = multiply_v(i)
+                nc.scalar.copy(
+                    out=plain_v[:, :, j, :], in_=v_bank[:].rearrange("p (h d) -> p h d", h=H)
+                )
+                if g == 0 and j == 0:
+                    x_grouped = operand_regroup(operand_flips(1))
+                if g == 0 and j == 1:
+                    x_quantise(GROUP, GROUP, x_grouped[:])
+                    reduce_angles(2, 2)
+                if j == 1 and g + 2 < GROUPS:
+                    x_grouped = operand_regroup(operand_flips(g + 2))
+                if 2 <= i < 2 + 4 * (B - 1):
+                    if (i - 2) % 4 == 0:
+                        table_steps = fill_table_steps((i - 2) // 4 + 1, 0, TILES_PER_BATCH)
+                    table_steps[(i - 2) % 4]()
+            store(out_2, b, t, GROUP, plain_v[:])
+            if g + 1 < GROUPS:
+                add(nc.gpsimd, rotated, DUO, shared, own, all_heads)
+                store(out_0, b, t, GROUP, rotated[:, q_heads])
+                store(out_1, b, t, GROUP, rotated[:, k_heads])
+            else:
+                for o, heads in ((out_0, q_heads), (out_1, k_heads)):
+                    store(o, b, t, DUO, rotated[:, heads, 0:DUO])
+                for o, heads in ((out_0, q_heads), (out_1, k_heads)):
+                    add(nc.vector, rotated, DUO, shared, own, heads)
+                    store(o, b, t + DUO, DUO, rotated[:, heads, DUO:GROUP])

@@ -40,8 +40,8 @@ def tile_ropeattention_pa_t_kernel(tc, x, coords, W_qkv, out_0, out_1, out_2):
         work = ctx.enter_context(tc.tile_pool(name="work", bufs=4))
         outs = ctx.enter_context(tc.tile_pool(name="outs", bufs=3))
         flip_pool = ctx.enter_context(tc.psum_pool(name="flips", bufs=2))
-        acc_pool = ctx.enter_context(tc.psum_pool(name="accs", bufs=4))
-        v_pool = ctx.enter_context(tc.psum_pool(name="vs", bufs=2))
+        acc_pool = ctx.enter_context(tc.psum_pool(name="accs", bufs=5))
+        v_pool = ctx.enter_context(tc.psum_pool(name="vs", bufs=1))
         ctx.enter_context(tc.manual_schedule())
 
         coords_sb = keep.tile([P, B, TILES_PER_BATCH, AXES], BF16)
@@ -93,23 +93,34 @@ def tile_ropeattention_pa_t_kernel(tc, x, coords, W_qkv, out_0, out_1, out_2):
         ANGLES = TILES_PER_BATCH * AXES
         fraction = keep.tile([P, B, ANGLES, FREQS], F32)
 
-        def reduce_angles(first, count):
+        def angle_steps(first, count):
             shape = [P, count * ANGLES, FREQS]
             turns = keep.tile(shape, F32, name="turns%d" % first)
             whole = keep.tile(shape, F32, name="whole%d" % first)
-            nc.vector.tensor_tensor(
-                out=turns[:],
-                in0=coords_sb[:, first : first + count].rearrange("p b t a -> p (b t a)").unsqueeze(2)
-                .to_broadcast(shape),
-                in1=turn_freqs[:].unsqueeze(1).to_broadcast(shape),
-                op=ALU.mult,
-            )
-            nc.vector.tensor_scalar(
-                out=whole[:], in0=turns[:], scalar1=ROUND_MAGIC, scalar2=ROUND_MAGIC,
-                op0=ALU.add, op1=ALU.subtract,
-            )
-            nc.vector.tensor_tensor(
-                out=fraction[:, first : first + count].rearrange("p b q j -> p (b q) j"), in0=turns[:], in1=whole[:], op=ALU.subtract)
+            batches = slice(first, first + count)
+
+            def scale():
+                nc.vector.tensor_tensor(
+                    out=turns[:],
+                    in0=coords_sb[:, batches].rearrange("p b t a -> p (b t a)").unsqueeze(2)
+                    .to_broadcast(shape),
+                    in1=turn_freqs[:].unsqueeze(1).to_broadcast(shape),
+                    op=ALU.mult,
+                )
+
+            def round_off():
+                nc.vector.tensor_scalar(
+                    out=whole[:], in0=turns[:], scalar1=ROUND_MAGIC, scalar2=ROUND_MAGIC,
+                    op0=ALU.add, op1=ALU.subtract,
+                )
+
+            def subtract():
+                nc.vector.tensor_tensor(
+                    out=fraction[:, batches].rearrange("p b q j -> p (b q) j"),
+                    in0=turns[:], in1=whole[:], op=ALU.subtract,
+                )
+
+            return [scale, round_off, subtract]
 
         def fill_table_steps(b, first, count):
             folded = stage.tile([P, TILES_PER_BATCH, 3, PAIRS], F32)
@@ -241,8 +252,8 @@ def tile_ropeattention_pa_t_kernel(tc, x, coords, W_qkv, out_0, out_1, out_2):
 
         q_heads, k_heads, all_heads = slice(0, H), slice(H, 2 * H), slice(0, 2 * H)
 
-        reduce_angles(0, 1)
-        reduce_angles(1, 1)
+        for step in angle_steps(0, 1):
+            step()
         w_grouped = [
             keep.tile([P, 2 * P * PACK], BF16, align_bytes=64, name="w_grouped%d" % n)
             for n in range(QK_BLOCKS)
@@ -253,20 +264,20 @@ def tile_ropeattention_pa_t_kernel(tc, x, coords, W_qkv, out_0, out_1, out_2):
             w_flips(bank, [wqk_words[:, n, e, :] for e in range(2)])
             w_banks.append(bank)
         x_banks = [x_flips(first) for first in range(0, GROUP, DUO)]
-        steps = fill_table_steps(0, 0, GROUP)
-        for step in steps[0:3]:
-            step()
-        regroup(nc.scalar.copy, w_grouped[0][:], w_banks[0], 2)
-        regroup(nc.vector.tensor_copy, w_grouped[1][:], w_banks[1], 2)
-        steps[3]()
-        w_quantise(w_grouped[0], (0, COLS))
-        regroup(nc.vector.tensor_copy, w_grouped[2][:], w_banks[2], 2)
-        w_quantise(w_grouped[1], (P, COLS + P))
-        w_quantise(w_grouped[2], (2 * P, COLS + 2 * P))
         x_grouped = stage.tile([P, GROUP * P * PACK], BF16, align_bytes=64, name="x_grouped")
+        half = DUO * P * PACK
+        regroup(nc.vector.tensor_copy, w_grouped[1][:], w_banks[1], 2)
+        for n in range(QK_BLOCKS):
+            if n != 1:
+                regroup(nc.scalar.copy, w_grouped[n][:], w_banks[n], 2)
+            if n == 0:
+                steps = fill_table_steps(0, 0, GROUP)
+                for step in steps[0:3]:
+                    step()
+            w_quantise(w_grouped[n], (n * P, COLS + n * P))
+        steps[3]()
         for duo, bank in enumerate(x_banks):
             x_regroup(x_grouped, duo, bank)
-        half = DUO * P * PACK
         x_quantise(0, DUO, x_grouped[:, 0:half])
         qk_banks = multiply_qk(0)
         v_grouped = [
@@ -279,6 +290,7 @@ def tile_ropeattention_pa_t_kernel(tc, x, coords, W_qkv, out_0, out_1, out_2):
             regroup(nc.scalar.copy, v_grouped[n][:, 0 : count * P * PACK], bank, count)
         for step in fill_table_steps(0, GROUP, GROUP):
             step()
+        late_angles = angle_steps(1, B - 1)
 
         def operand_flips(g):
             return [x_flips(g * GROUP + duo) for duo in range(0, GROUP, DUO)]
@@ -306,9 +318,9 @@ def tile_ropeattention_pa_t_kernel(tc, x, coords, W_qkv, out_0, out_1, out_2):
                 for step in steps[0:2]:
                     step()
                 if j == GROUP - 1:
-                    add(nc.vector, rotated, 0, early[0], early[1], all_heads)
                     if g + 2 < GROUPS:
                         x_quantise((g + 2) * GROUP, GROUP, x_grouped[:])
+                    add(nc.vector, rotated, 0, early[0], early[1], all_heads)
                 steps[2]()
                 if g == 0 and j == 0:
                     x_quantise(DUO, DUO, x_grouped[:, half : 2 * half])
@@ -316,21 +328,24 @@ def tile_ropeattention_pa_t_kernel(tc, x, coords, W_qkv, out_0, out_1, out_2):
                     w_quantise(v_grouped[1], (2 * COLS + 2 * P,))
                 if i + 1 < TILES:
                     qk_banks = multiply_qk(i + 1)
+                if j == GROUP - 1 and g + 3 < GROUPS:
+                    x_banks = operand_flips(g + 3)
                 v_bank = multiply_v(i)
                 nc.scalar.copy(
                     out=plain_v[:, :, j, :], in_=v_bank[:].rearrange("p (h d) -> p h d", h=H)
                 )
-                if g == 0 and j == 0:
-                    x_grouped = operand_regroup(operand_flips(1))
-                if g == 0 and j == 1:
-                    x_quantise(GROUP, GROUP, x_grouped[:])
-                    reduce_angles(2, 2)
-                if j == 1 and g + 2 < GROUPS:
-                    x_grouped = operand_regroup(operand_flips(g + 2))
-                if 2 <= i < 2 + 4 * (B - 1):
-                    if (i - 2) % 4 == 0:
-                        table_steps = fill_table_steps((i - 2) // 4 + 1, 0, TILES_PER_BATCH)
-                    table_steps[(i - 2) % 4]()
+                if g == 0 and j < 2:
+                    if j == 1:
+                        x_quantise(GROUP, GROUP, x_grouped[:])
+                    x_grouped = operand_regroup(operand_flips(j + 1))
+                if j == GROUP - 1 and g + 3 < GROUPS:
+                    x_grouped = operand_regroup(x_banks)
+                if g == 0 and j < GROUP - 1:
+                    late_angles[j]()
+                if 3 <= i < 3 + 4 * (B - 1):
+                    if (i - 3) % 4 == 0:
+                        table_steps = fill_table_steps((i - 3) // 4 + 1, 0, TILES_PER_BATCH)
+                    table_steps[(i - 3) % 4]()
             store(out_2, b, t, GROUP, plain_v[:])
             if g + 1 < GROUPS:
                 add(nc.gpsimd, rotated, DUO, shared, own, all_heads)

@@ -37,7 +37,7 @@ def tile_ropeattention_pa_t_kernel(tc, x, coords, W_qkv, out_0, out_1, out_2):
     with ExitStack() as ctx:
         keep = ctx.enter_context(tc.tile_pool(name="keep", bufs=1))
         stage = ctx.enter_context(tc.tile_pool(name="stage", bufs=2))
-        work = ctx.enter_context(tc.tile_pool(name="work", bufs=4))
+        work = ctx.enter_context(tc.tile_pool(name="work", bufs=2))
         outs = ctx.enter_context(tc.tile_pool(name="outs", bufs=3))
         flip_pool = ctx.enter_context(tc.psum_pool(name="flips", bufs=2))
         acc_pool = ctx.enter_context(tc.psum_pool(name="accs", bufs=5))
@@ -45,7 +45,7 @@ def tile_ropeattention_pa_t_kernel(tc, x, coords, W_qkv, out_0, out_1, out_2):
         ctx.enter_context(tc.manual_schedule())
 
         coords_sb = keep.tile([P, B, TILES_PER_BATCH, AXES], BF16)
-        nc.scalar.dma_start(
+        nc.sync.dma_start(
             out=coords_sb[:], in_=coords.rearrange("b (p t) a -> p b t a", t=TILES_PER_BATCH)
         )
         wqk_sb = keep.tile([P, QK_BLOCKS, 2, D], BF16)
@@ -95,8 +95,8 @@ def tile_ropeattention_pa_t_kernel(tc, x, coords, W_qkv, out_0, out_1, out_2):
 
         def angle_steps(first, count):
             shape = [P, count * ANGLES, FREQS]
-            turns = keep.tile(shape, F32, name="turns%d" % first)
-            whole = keep.tile(shape, F32, name="whole%d" % first)
+            turns = stage.tile(shape, F32, name="turns", bufs=1)
+            whole = stage.tile(shape, F32, name="whole", bufs=1)
             batches = slice(first, first + count)
 
             def scale():
@@ -232,17 +232,18 @@ def tile_ropeattention_pa_t_kernel(tc, x, coords, W_qkv, out_0, out_1, out_2):
                 )
 
             return [
-                partial(product, banks[0], 1, root2, own[:, :, slot, 1, :]),
-                partial(product, banks[1], 2, root2, own[:, :, slot, 0, :]),
-                partial(product, banks[2], 0, -1.0, shared[:, :, slot, :]),
+                partial(product, banks[0], 1, root2, own[:, slot, :, 1, :]),
+                partial(product, banks[1], 2, root2, own[:, slot, :, 0, :]),
+                partial(product, banks[2], 0, -1.0, shared[:, slot]),
             ]
 
-        def add(engine, rotated, j, shared, own, heads):
-            count = heads.stop - heads.start
+        def add(engine, rotated, shared, own, heads, tiles):
+            count = tiles.stop - tiles.start
             engine.tensor_tensor(
-                out=rotated[:, heads, j : j + DUO, :].rearrange("p m j (n e) -> p m j n e", e=2),
-                in0=shared[:, heads].unsqueeze(4).to_broadcast([P, count, DUO, PAIRS, 2]),
-                in1=own[:, heads].rearrange("p m j e n -> p m j n e"),
+                out=rotated[:, heads, tiles, :].rearrange("p m j (n e) -> p j m n e", e=2),
+                in0=shared[:, tiles, heads].unsqueeze(4)
+                .to_broadcast([P, count, heads.stop - heads.start, PAIRS, 2]),
+                in1=own[:, tiles, heads].rearrange("p j m e n -> p j m n e"),
                 op=ALU.add,
             )
 
@@ -250,10 +251,21 @@ def tile_ropeattention_pa_t_kernel(tc, x, coords, W_qkv, out_0, out_1, out_2):
             view = o[b].rearrange("h (p t) d -> p h t d", t=TILES_PER_BATCH)
             nc.sync.dma_start(out=view[:, :, t : t + count, :], in_=tile)
 
+        V_PARTS = ((0, 2), (2, 1))
+        GROUPS = TILES // GROUP
         q_heads, k_heads, all_heads = slice(0, H), slice(H, 2 * H), slice(0, 2 * H)
 
-        for step in angle_steps(0, 1):
-            step()
+        def vector_adds(g):
+            if g < GROUPS - 2:
+                return {GROUP - 1: slice(0, 1)}
+            if g < GROUPS - 1:
+                return {GROUP - 1: slice(0, 2)}
+            return {GROUP - 2: slice(0, 2), GROUP - 1: slice(2, 3)}
+
+        for b in range(2):
+            for step in angle_steps(b, 1):
+                step()
+        late_angles = angle_steps(2, B - 2)
         w_grouped = [
             keep.tile([P, 2 * P * PACK], BF16, align_bytes=64, name="w_grouped%d" % n)
             for n in range(QK_BLOCKS)
@@ -263,69 +275,77 @@ def tile_ropeattention_pa_t_kernel(tc, x, coords, W_qkv, out_0, out_1, out_2):
             bank = acc_pool.tile([P, 2, 2, P], F32, name="bank")
             w_flips(bank, [wqk_words[:, n, e, :] for e in range(2)])
             w_banks.append(bank)
-        x_banks = [x_flips(first) for first in range(0, GROUP, DUO)]
-        x_grouped = stage.tile([P, GROUP * P * PACK], BF16, align_bytes=64, name="x_grouped")
-        half = DUO * P * PACK
-        regroup(nc.vector.tensor_copy, w_grouped[1][:], w_banks[1], 2)
-        for n in range(QK_BLOCKS):
-            if n != 1:
-                regroup(nc.scalar.copy, w_grouped[n][:], w_banks[n], 2)
-            if n == 0:
-                steps = fill_table_steps(0, 0, GROUP)
-                for step in steps[0:3]:
-                    step()
-            w_quantise(w_grouped[n], (n * P, COLS + n * P))
-        steps[3]()
-        for duo, bank in enumerate(x_banks):
-            x_regroup(x_grouped, duo, bank)
-        x_quantise(0, DUO, x_grouped[:, 0:half])
-        qk_banks = multiply_qk(0)
+        x_banks = [x_flips(0)]
         v_grouped = [
             keep.tile([P, 2 * P * PACK], BF16, align_bytes=64, name="v_grouped%d" % n)
             for n in range(2)
         ]
-        for n, (first, count) in enumerate(((0, 2), (2, 1))):
-            bank = v_pool.tile([P, 2, 2, P], F32, name="v_bank")
+        v_banks = []
+        for first, count in V_PARTS:
+            bank = acc_pool.tile([P, 2, 2, P], F32, name="bank")
             w_flips(bank, [wv_words[:, first + s, :] for s in range(count)])
-            regroup(nc.scalar.copy, v_grouped[n][:, 0 : count * P * PACK], bank, count)
-        for step in fill_table_steps(0, GROUP, GROUP):
+            v_banks.append(bank)
+        x_grouped = stage.tile([P, GROUP * P * PACK], BF16, align_bytes=64, name="x_grouped", bufs=3)
+        half = DUO * P * PACK
+        steps = fill_table_steps(0, 0, GROUP)
+        regroup(nc.scalar.copy, w_grouped[0][:], w_banks[0], 2)
+        for step in steps[0:3]:
             step()
-        late_angles = angle_steps(1, B - 1)
+        for n in range(1, QK_BLOCKS):
+            regroup(nc.vector.tensor_copy, w_grouped[n][:], w_banks[n], 2)
+        x_regroup(x_grouped, 0, x_banks[0])
+        steps[3]()
+        for n in range(QK_BLOCKS):
+            w_quantise(w_grouped[n], (n * P, COLS + n * P))
+        x_quantise(0, DUO, x_grouped[:, 0:half])
+        late_angles[0]()
+        qk_banks = multiply_qk(0)
+        x_banks.append(x_flips(DUO))
+        for n, (first, count) in enumerate(V_PARTS):
+            regroup(nc.scalar.copy, v_grouped[n][:, 0 : count * P * PACK], v_banks[n], count)
+        x_regroup(x_grouped, 1, x_banks[1])
+
+        first_x = x_grouped
 
         def operand_flips(g):
             return [x_flips(g * GROUP + duo) for duo in range(0, GROUP, DUO)]
 
         def operand_regroup(banks):
-            grouped = stage.tile([P, GROUP * P * PACK], BF16, align_bytes=64, name="x_grouped")
+            grouped = stage.tile([P, GROUP * P * PACK], BF16, align_bytes=64, name="x_grouped", bufs=3)
             for duo, bank in enumerate(banks):
                 x_regroup(grouped, duo, bank)
             return grouped
 
-        GROUPS = TILES // GROUP
         for g in range(GROUPS):
             b, t = divmod(g * GROUP, TILES_PER_BATCH)
             rotated = outs.tile([P, 2 * H, GROUP, HD], F32)
             plain_v = outs.tile([P, H, GROUP, HD], F32)
+            shared = work.tile([P, GROUP, 2 * H, PAIRS], F32)
+            own = work.tile([P, GROUP, 2 * H, 2, PAIRS], F32)
             for j in range(GROUP):
                 i = g * GROUP + j
-                slot = j % DUO
-                if slot == 0:
-                    shared = work.tile([P, 2 * H, DUO, PAIRS], F32)
-                    own = work.tile([P, 2 * H, DUO, 2, PAIRS], F32)
-                if j == 0:
-                    early = (shared, own)
-                steps = product_steps(i, qk_banks, slot, shared, own)
+                steps = product_steps(i, qk_banks, j, shared, own)
                 for step in steps[0:2]:
                     step()
-                if j == GROUP - 1:
-                    if g + 2 < GROUPS:
-                        x_quantise((g + 2) * GROUP, GROUP, x_grouped[:])
-                    add(nc.vector, rotated, 0, early[0], early[1], all_heads)
+                if j == GROUP - 1 and g + 2 < GROUPS:
+                    x_quantise((g + 2) * GROUP, GROUP, x_grouped[:])
+                tiles = vector_adds(g).get(j)
+                if tiles is not None:
+                    add(nc.vector, rotated, shared, own, all_heads, tiles)
+                if g == GROUPS - 1 and j == GROUP - 2:
+                    store(out_2, b, t, DUO, plain_v[:, :, 0:DUO])
+                    for o, heads in ((out_0, q_heads), (out_1, k_heads)):
+                        store(o, b, t, DUO, rotated[:, heads, 0:DUO])
                 steps[2]()
                 if g == 0 and j == 0:
-                    x_quantise(DUO, DUO, x_grouped[:, half : 2 * half])
                     w_quantise(v_grouped[0], (2 * COLS, 2 * COLS + P))
                     w_quantise(v_grouped[1], (2 * COLS + 2 * P,))
+                if g == 0 and j == 1:
+                    x_quantise(DUO, DUO, first_x[:, half : 2 * half])
+                    late_angles[1]()
+                if g == 0 and j == 2:
+                    x_quantise(GROUP, GROUP, second_x[:])
+                    late_angles[2]()
                 if i + 1 < TILES:
                     qk_banks = multiply_qk(i + 1)
                 if j == GROUP - 1 and g + 3 < GROUPS:
@@ -336,24 +356,25 @@ def tile_ropeattention_pa_t_kernel(tc, x, coords, W_qkv, out_0, out_1, out_2):
                 )
                 if g == 0 and j < 2:
                     if j == 1:
-                        x_quantise(GROUP, GROUP, x_grouped[:])
+                        second_x = x_grouped
                     x_grouped = operand_regroup(operand_flips(j + 1))
+                    if j == 0:
+                        for step in fill_table_steps(0, GROUP, GROUP):
+                            step()
                 if j == GROUP - 1 and g + 3 < GROUPS:
                     x_grouped = operand_regroup(x_banks)
-                if g == 0 and j < GROUP - 1:
-                    late_angles[j]()
                 if 3 <= i < 3 + 4 * (B - 1):
                     if (i - 3) % 4 == 0:
                         table_steps = fill_table_steps((i - 3) // 4 + 1, 0, TILES_PER_BATCH)
                     table_steps[(i - 3) % 4]()
-            store(out_2, b, t, GROUP, plain_v[:])
-            if g + 1 < GROUPS:
-                add(nc.gpsimd, rotated, DUO, shared, own, all_heads)
-                store(out_0, b, t, GROUP, rotated[:, q_heads])
-                store(out_1, b, t, GROUP, rotated[:, k_heads])
+            if g < GROUPS - 1:
+                store(out_2, b, t, GROUP, plain_v[:])
+                pool_tiles = slice(vector_adds(g)[GROUP - 1].stop, GROUP)
+                add(nc.gpsimd, rotated, shared, own, all_heads, pool_tiles)
+                for o, heads in ((out_0, q_heads), (out_1, k_heads)):
+                    store(o, b, t, GROUP, rotated[:, heads])
             else:
+                store(out_2, b, t + DUO, DUO, plain_v[:, :, DUO:GROUP])
                 for o, heads in ((out_0, q_heads), (out_1, k_heads)):
-                    store(o, b, t, DUO, rotated[:, heads, 0:DUO])
-                for o, heads in ((out_0, q_heads), (out_1, k_heads)):
-                    add(nc.vector, rotated, DUO, shared, own, heads)
+                    add(nc.vector, rotated, shared, own, heads, slice(GROUP - 1, GROUP))
                     store(o, b, t + DUO, DUO, rotated[:, heads, DUO:GROUP])

@@ -256,8 +256,6 @@ def tile_ropeattention_pa_t_kernel(tc, x, coords, W_qkv, out_0, out_1, out_2):
         q_heads, k_heads, all_heads = slice(0, H), slice(H, 2 * H), slice(0, 2 * H)
 
         def vector_adds(g):
-            if g < GROUPS - 2:
-                return {GROUP - 1: slice(0, 1)}
             if g < GROUPS - 1:
                 return {GROUP - 1: slice(0, 2)}
             return {GROUP - 2: slice(0, 2), GROUP - 1: slice(2, 3)}
@@ -316,10 +314,31 @@ def tile_ropeattention_pa_t_kernel(tc, x, coords, W_qkv, out_0, out_1, out_2):
                 x_regroup(grouped, duo, bank)
             return grouped
 
+        v_done = []
+        plain_v = []
+
+        def v_turns(i):
+            if len(v_done) == TILES:
+                return 0
+            return 2 if i % GROUP == 2 and 2 <= i // GROUP < 6 else 1
+
+        def project_v():
+            i = len(v_done)
+            b, t = divmod(i, TILES_PER_BATCH)
+            j = i % GROUP
+            if j == 0:
+                plain_v.append(outs.tile([P, H, GROUP, HD], F32, name="plain_v"))
+            v_bank = multiply_v(i)
+            nc.scalar.copy(
+                out=plain_v[-1][:, :, j, :], in_=v_bank[:].rearrange("p (h d) -> p h d", h=H)
+            )
+            if j == GROUP - 1:
+                store(out_2, b, t - j, GROUP, plain_v[-1][:])
+            v_done.append(i)
+
         for g in range(GROUPS):
             b, t = divmod(g * GROUP, TILES_PER_BATCH)
             rotated = outs.tile([P, 2 * H, GROUP, HD], F32)
-            plain_v = outs.tile([P, H, GROUP, HD], F32)
             shared = work.tile([P, GROUP, 2 * H, PAIRS], F32)
             own = work.tile([P, GROUP, 2 * H, 2, PAIRS], F32)
             for j in range(GROUP):
@@ -333,7 +352,6 @@ def tile_ropeattention_pa_t_kernel(tc, x, coords, W_qkv, out_0, out_1, out_2):
                 if tiles is not None:
                     add(nc.vector, rotated, shared, own, all_heads, tiles)
                 if g == GROUPS - 1 and j == GROUP - 2:
-                    store(out_2, b, t, DUO, plain_v[:, :, 0:DUO])
                     for o, heads in ((out_0, q_heads), (out_1, k_heads)):
                         store(o, b, t, DUO, rotated[:, heads, 0:DUO])
                 steps[2]()
@@ -350,10 +368,8 @@ def tile_ropeattention_pa_t_kernel(tc, x, coords, W_qkv, out_0, out_1, out_2):
                     qk_banks = multiply_qk(i + 1)
                 if j == GROUP - 1 and g + 3 < GROUPS:
                     x_banks = operand_flips(g + 3)
-                v_bank = multiply_v(i)
-                nc.scalar.copy(
-                    out=plain_v[:, :, j, :], in_=v_bank[:].rearrange("p (h d) -> p h d", h=H)
-                )
+                for n in range(v_turns(i)):
+                    project_v()
                 if g == 0 and j < 2:
                     if j == 1:
                         second_x = x_grouped
@@ -368,13 +384,16 @@ def tile_ropeattention_pa_t_kernel(tc, x, coords, W_qkv, out_0, out_1, out_2):
                         table_steps = fill_table_steps((i - 3) // 4 + 1, 0, TILES_PER_BATCH)
                     table_steps[(i - 3) % 4]()
             if g < GROUPS - 1:
-                store(out_2, b, t, GROUP, plain_v[:])
                 pool_tiles = slice(vector_adds(g)[GROUP - 1].stop, GROUP)
                 add(nc.gpsimd, rotated, shared, own, all_heads, pool_tiles)
-                for o, heads in ((out_0, q_heads), (out_1, k_heads)):
-                    store(o, b, t, GROUP, rotated[:, heads])
+                if g < GROUPS - 2:
+                    for o, heads in ((out_0, q_heads), (out_1, k_heads)):
+                        store(o, b, t, GROUP, rotated[:, heads])
+                else:
+                    for first in (0, DUO):
+                        for o, heads in ((out_0, q_heads), (out_1, k_heads)):
+                            store(o, b, t + first, DUO, rotated[:, heads, first : first + DUO])
             else:
-                store(out_2, b, t + DUO, DUO, plain_v[:, :, DUO:GROUP])
                 for o, heads in ((out_0, q_heads), (out_1, k_heads)):
                     add(nc.vector, rotated, shared, own, heads, slice(GROUP - 1, GROUP))
                     store(o, b, t + DUO, DUO, rotated[:, heads, DUO:GROUP])

import math
from contextlib import ExitStack
from functools import partial

import concourse.mybir as mybir
from concourse.masks import make_identity

F32 = mybir.dt.float32
BF16 = mybir.dt.bfloat16
U32 = mybir.dt.uint32
U8 = mybir.dt.uint8
FP8X4 = mybir.dt.float8_e4m3fn_x4
ALU = mybir.AluOpType
ACT = mybir.ActivationFunctionType

P = 128
PACK = 4
B, S, D, H, HD = 4, 1024, 512, 4, 96
PAIRS = HD // 2
AXES = 3
FREQS = PAIRS // AXES
COLS = H * HD
TILES_PER_BATCH = S // P
TILES = B * TILES_PER_BATCH
QK_BLOCKS = 2 * COLS // (2 * P)
V_BLOCKS = COLS // P
WORDS = D // 2
GROUP = 4
DUO = 2
ROUND_MAGIC = 1.5 * 2.0**23

FLOPS = 2 * B * S * D * 3 * COLS


def tile_ropeattention_pa_t_kernel(tc, x, coords, W_qkv, out_0, out_1, out_2):
    nc = tc.nc
    with ExitStack() as ctx:
        keep = ctx.enter_context(tc.tile_pool(name="keep", bufs=1))
        stage = ctx.enter_context(tc.tile_pool(name="stage", bufs=2))
        work = ctx.enter_context(tc.tile_pool(name="work", bufs=2))
        outs = ctx.enter_context(tc.tile_pool(name="outs", bufs=3))
        flip_pool = ctx.enter_context(tc.psum_pool(name="flips", bufs=2))
        acc_pool = ctx.enter_context(tc.psum_pool(name="accs", bufs=5))
        v_pool = ctx.enter_context(tc.psum_pool(name="vs", bufs=1))
        ctx.enter_context(tc.manual_schedule())

        coords_sb = keep.tile([P, B, TILES_PER_BATCH, AXES], BF16)
        nc.sync.dma_start(
            out=coords_sb[:], in_=coords.rearrange("b (p t) a -> p b t a", t=TILES_PER_BATCH)
        )
        wqk_sb = keep.tile([P, QK_BLOCKS, 2, D], BF16)
        wqk_rows = W_qkv[0 : 2 * COLS].rearrange("(n p e) k -> n p e k", p=P, e=2)
        wv_sb = keep.tile([P, V_BLOCKS, D], BF16)
        wv_rows = W_qkv[2 * COLS : 3 * COLS].rearrange("(n p) k -> p n k", p=P)
        x_sb = keep.tile([P, B, TILES_PER_BATCH, D], BF16)
        x_rows = x.rearrange("b (p t) k -> b p t k", t=TILES_PER_BATCH)
        for n in range(QK_BLOCKS):
            nc.sync.dma_start(out=wqk_sb[:, n], in_=wqk_rows[n])
        for t in range(0, GROUP, DUO):
            nc.sync.dma_start(out=x_sb[:, 0, t : t + DUO], in_=x_rows[0, :, t : t + DUO])
        nc.sync.dma_start(out=wv_sb[:], in_=wv_rows)
        nc.sync.dma_start(out=x_sb[:, 0, GROUP:], in_=x_rows[0, :, GROUP:])
        for b in range(1, B):
            nc.sync.dma_start(out=x_sb[:, b], in_=x_rows[b])

        identity = keep.tile([P, P], F32)
        make_identity(nc, identity[:])

        ones = keep.tile([P, 1], F32)
        nc.vector.memset(ones[:], 1.0)
        turn_freqs = keep.tile([P, FREQS], F32)
        nc.vector.tensor_scalar(
            out=turn_freqs[:, 0:1], in0=ones[:],
            scalar1=1.0 / (2.0 * math.pi), scalar2=None, op0=ALU.mult,
        )
        filled = 1
        while filled < FREQS:
            nc.vector.tensor_scalar(
                out=turn_freqs[:, filled : 2 * filled], in0=turn_freqs[:, 0:filled],
                scalar1=10000.0 ** (-filled / FREQS), scalar2=None, op0=ALU.mult,
            )
            filled *= 2
        biases = keep.tile([P, 4], F32)
        for w, value in enumerate((0.0, 0.25, -0.25, -0.5)):
            nc.vector.tensor_scalar(
                out=biases[:, w : w + 1], in0=ones[:],
                scalar1=value * math.pi, scalar2=None, op0=ALU.mult,
            )
        warm = keep.tile([P, 1], F32)
        nc.scalar.activation(out=warm[:], in_=ones[:], func=ACT.Sin)

        table = keep.tile([P, TILES, 3, PAIRS], F32)
        ANGLES = TILES_PER_BATCH * AXES
        fraction = keep.tile([P, B, ANGLES, FREQS], F32)

        def angle_steps(first, count):
            shape = [P, count * ANGLES, FREQS]
            turns = stage.tile(shape, F32, name="turns", bufs=1)
            whole = stage.tile(shape, F32, name="whole", bufs=1)
            batches = slice(first, first + count)

            def scale():
                nc.vector.tensor_tensor(
                    out=turns[:],
                    in0=coords_sb[:, batches].rearrange("p b t a -> p (b t a)").unsqueeze(2)
                    .to_broadcast(shape),
                    in1=turn_freqs[:].unsqueeze(1).to_broadcast(shape),
                    op=ALU.mult,
                )

            def round_off():
                nc.vector.tensor_scalar(
                    out=whole[:], in0=turns[:], scalar1=ROUND_MAGIC, scalar2=ROUND_MAGIC,
                    op0=ALU.add, op1=ALU.subtract,
                )

            def subtract():
                nc.vector.tensor_tensor(
                    out=fraction[:, batches].rearrange("p b q j -> p (b q) j"),
                    in0=turns[:], in1=whole[:], op=ALU.subtract,
                )

            return [scale, round_off, subtract]

        def fill_table_steps(b, first, count):
            folded = stage.tile([P, TILES_PER_BATCH, 3, PAIRS], F32)
            angles = fraction[:, b].rearrange("p (t a) j -> p t (a j)", a=AXES)

            def fold(w):
                nc.scalar.activation(
                    out=folded[:, 0:count, w, :], in_=angles[:, first : first + count],
                    func=ACT.Abs, scale=2.0 * math.pi, bias=biases[:, w : w + 1],
                )

            def sines():
                i = b * TILES_PER_BATCH + first
                nc.scalar.activation(
                    out=table[:, i : i + count], in_=folded[:, 0:count],
                    func=ACT.Sin, bias=biases[:, 3:4],
                )

            return [partial(fold, 0), partial(fold, 1), partial(fold, 2), sines]

        def flip(bank, slot, rows):
            for u in range(2):
                nc.tensor.transpose(bank[:, slot, u, :], rows[:, u:WORDS:2], identity[:])

        def regroup(copy, grouped, bank, slots):
            copy(
                out=grouped.bitcast(F32).rearrange("p (i r u) -> p i r u", r=P, u=2),
                in_=bank[:, 0:slots].rearrange("p i u r -> p i r u"),
            )

        w_codes = keep.tile([P, 3 * COLS], U32, align_bytes=64)
        w_scales = keep.tile([P, 3 * COLS], U8, align_bytes=64)
        x_codes = keep.tile([P, TILES * P], U32, align_bytes=64)
        x_scales = keep.tile([P, TILES * P], U8, align_bytes=64)
        wqk_words = wqk_sb[:].bitcast(F32)
        wv_words = wv_sb[:].bitcast(F32)
        x_words = x_sb[:].bitcast(F32)

        def quantise(codes, scales, grouped):
            nc.vector.quantize_mx(out=codes.bitcast(FP8X4), scales=scales, in_=grouped)

        def w_flips(bank, tiles):
            for slot, rows in enumerate(tiles):
                flip(bank, slot, rows)
            return bank

        def w_quantise(grouped, columns):
            for slot, first in enumerate(columns):
                cols = slice(first, first + P)
                quantise(
                    w_codes[:, cols], w_scales[:, cols],
                    grouped[:, slot * P * PACK : (slot + 1) * P * PACK],
                )

        def x_flips(first):
            b, t = divmod(first, TILES_PER_BATCH)
            bank = flip_pool.tile([P, DUO, 2, P], F32, name="flip")
            for slot in range(DUO):
                flip(bank, slot, x_words[:, b, t + slot, :])
            return bank

        def x_regroup(grouped, duo, bank):
            columns = slice(duo * DUO * P * PACK, (duo + 1) * DUO * P * PACK)
            regroup(nc.scalar.copy, grouped[:, columns], bank, DUO)

        def x_quantise(first, count, grouped):
            cols = slice(first * P, (first + count) * P)
            quantise(x_codes[:, cols], x_scales[:, cols], grouped)

        def passes(bank, i, col0s):
            tokens = slice(i * P, (i + 1) * P)
            for lo, width in ((0, 256), (256, 128)):
                for n, col0 in enumerate(col0s):
                    cols = slice(col0 + lo, col0 + lo + width)
                    nc.tensor.matmul_mx(
                        out=bank[:, lo : lo + width],
                        lhsT=x_codes[:, tokens].bitcast(FP8X4),
                        lhsT_scale=x_scales[:, tokens],
                        rhs=w_codes[:, cols].bitcast(FP8X4),
                        rhs_scale=w_scales[:, cols],
                        start=(n == 0),
                        stop=(n == len(col0s) - 1),
                    )

        def multiply_qk(i):
            banks = []
            for col0s in ((0,), (COLS,), (0, COLS)):
                bank = acc_pool.tile([P, COLS], F32, name="bank")
                passes(bank, i, col0s)
                banks.append(bank)
            return banks

        def multiply_v(i):
            v_bank = v_pool.tile([P, COLS], F32, name="v_bank")
            passes(v_bank, i, (2 * COLS,))
            return v_bank

        def product_steps(i, banks, slot, shared, own):
            root2 = math.sqrt(2.0)

            def product(bank, w, factor, out):
                nc.vector.scalar_tensor_tensor(
                    out=out,
                    in0=bank[:].rearrange("p (m n) -> p m n", m=2 * H),
                    scalar=factor,
                    in1=table[:, i, w, :].unsqueeze(1).to_broadcast([P, 2 * H, PAIRS]),
                    op0=ALU.mult,
                    op1=ALU.mult,
                )

            return [
                partial(product, banks[0], 1, root2, own[:, slot, :, 1, :]),
                partial(product, banks[1], 2, root2, own[:, slot, :, 0, :]),
                partial(product, banks[2], 0, -1.0, shared[:, slot]),
            ]

        def add(engine, rotated, shared, own, heads, tiles):
            count = tiles.stop - tiles.start
            engine.tensor_tensor(
                out=rotated[:, heads, tiles, :].rearrange("p m j (n e) -> p j m n e", e=2),
                in0=shared[:, tiles, heads].unsqueeze(4)
                .to_broadcast([P, count, heads.stop - heads.start, PAIRS, 2]),
                in1=own[:, tiles, heads].rearrange("p j m e n -> p j m n e"),
                op=ALU.add,
            )

        def store(o, b, t, count, tile):
            view = o[b].rearrange("h (p t) d -> p h t d", t=TILES_PER_BATCH)
            nc.sync.dma_start(out=view[:, :, t : t + count, :], in_=tile)

        V_PARTS = ((0, 2), (2, 1))
        GROUPS = TILES // GROUP
        q_heads, k_heads, all_heads = slice(0, H), slice(H, 2 * H), slice(0, 2 * H)

        def vector_adds(g):
            if g < GROUPS - 1:
                return {GROUP - 1: slice(0, 2)}
            return {GROUP - 2: slice(0, 2), GROUP - 1: slice(2, 3)}

        for b in range(2):
            for step in angle_steps(b, 1):
                step()
        late_angles = angle_steps(2, B - 2)
        w_grouped = [
            keep.tile([P, 2 * P * PACK], BF16, align_bytes=64, name="w_grouped%d" % n)
            for n in range(QK_BLOCKS)
        ]
        w_banks = []
        for n in range(QK_BLOCKS):
            bank = acc_pool.tile([P, 2, 2, P], F32, name="bank")
            w_flips(bank, [wqk_words[:, n, e, :] for e in range(2)])
            w_banks.append(bank)
        x_banks = [x_flips(0)]
        v_grouped = [
            keep.tile([P, 2 * P * PACK], BF16, align_bytes=64, name="v_grouped%d" % n)
            for n in range(2)
        ]
        v_banks = []
        for first, count in V_PARTS:
            bank = acc_pool.tile([P, 2, 2, P], F32, name="bank")
            w_flips(bank, [wv_words[:, first + s, :] for s in range(count)])
            v_banks.append(bank)
        x_grouped = stage.tile([P, GROUP * P * PACK], BF16, align_bytes=64, name="x_grouped", bufs=3)
        half = DUO * P * PACK
        steps = fill_table_steps(0, 0, GROUP)
        regroup(nc.scalar.copy, w_grouped[0][:], w_banks[0], 2)
        for step in steps[0:3]:
            step()
        for n in range(1, QK_BLOCKS):
            regroup(nc.vector.tensor_copy, w_grouped[n][:], w_banks[n], 2)
        x_regroup(x_grouped, 0, x_banks[0])
        steps[3]()
        for n in range(QK_BLOCKS):
            w_quantise(w_grouped[n], (n * P, COLS + n * P))
        x_quantise(0, DUO, x_grouped[:, 0:half])
        late_angles[0]()
        qk_banks = multiply_qk(0)
        x_banks.append(x_flips(DUO))
        for n, (first, count) in enumerate(V_PARTS):
            regroup(nc.scalar.copy, v_grouped[n][:, 0 : count * P * PACK], v_banks[n], count)
        x_regroup(x_grouped, 1, x_banks[1])

        first_x = x_grouped

        def operand_flips(g):
            return [x_flips(g * GROUP + duo) for duo in range(0, GROUP, DUO)]

        def operand_regroup(banks):
            grouped = stage.tile([P, GROUP * P * PACK], BF16, align_bytes=64, name="x_grouped", bufs=3)
            for duo, bank in enumerate(banks):
                x_regroup(grouped, duo, bank)
            return grouped

        v_done = []
        plain_v = []

        def v_turns(i):
            if len(v_done) == TILES:
                return 0
            return 2 if i % GROUP == 2 and 2 <= i // GROUP < 6 else 1

        def project_v():
            i = len(v_done)
            b, t = divmod(i, TILES_PER_BATCH)
            j = i % GROUP
            if j == 0:
                plain_v.append(outs.tile([P, H, GROUP, HD], F32, name="plain_v"))
            v_bank = multiply_v(i)
            nc.scalar.copy(
                out=plain_v[-1][:, :, j, :], in_=v_bank[:].rearrange("p (h d) -> p h d", h=H)
            )
            if j == GROUP - 1:
                store(out_2, b, t - j, GROUP, plain_v[-1][:])
            v_done.append(i)

        for g in range(GROUPS):
            b, t = divmod(g * GROUP, TILES_PER_BATCH)
            rotated = outs.tile([P, 2 * H, GROUP, HD], F32)
            shared = work.tile([P, GROUP, 2 * H, PAIRS], F32)
            own = work.tile([P, GROUP, 2 * H, 2, PAIRS], F32)
            for j in range(GROUP):
                i = g * GROUP + j
                steps = product_steps(i, qk_banks, j, shared, own)
                for step in steps[0:2]:
                    step()
                if j == GROUP - 1 and g + 2 < GROUPS:
                    x_quantise((g + 2) * GROUP, GROUP, x_grouped[:])
                tiles = vector_adds(g).get(j)
                if tiles is not None:
                    add(nc.vector, rotated, shared, own, all_heads, tiles)
                if g == GROUPS - 1 and j == GROUP - 2:
                    for o, heads in ((out_0, q_heads), (out_1, k_heads)):
                        store(o, b, t, DUO, rotated[:, heads, 0:DUO])
                steps[2]()
                if g == 0 and j == 0:
                    w_quantise(v_grouped[0], (2 * COLS, 2 * COLS + P))
                    w_quantise(v_grouped[1], (2 * COLS + 2 * P,))
                if g == 0 and j == 1:
                    x_quantise(DUO, DUO, first_x[:, half : 2 * half])
                    late_angles[1]()
                if g == 0 and j == 2:
                    x_quantise(GROUP, GROUP, second_x[:])
                    late_angles[2]()
                if i + 1 < TILES:
                    qk_banks = multiply_qk(i + 1)
                if j == GROUP - 1 and g + 3 < GROUPS:
                    x_banks = operand_flips(g + 3)
                for n in range(v_turns(i)):
                    project_v()
                if g == 0 and j < 2:
                    if j == 1:
                        second_x = x_grouped
                    x_grouped = operand_regroup(operand_flips(j + 1))
                    if j == 0:
                        for step in fill_table_steps(0, GROUP, GROUP):
                            step()
                if j == GROUP - 1 and g + 3 < GROUPS:
                    x_grouped = operand_regroup(x_banks)
                if 3 <= i < 3 + 4 * (B - 1):
                    if (i - 3) % 4 == 0:
                        table_steps = fill_table_steps((i - 3) // 4 + 1, 0, TILES_PER_BATCH)
                    table_steps[(i - 3) % 4]()
            if g < GROUPS - 1:
                pool_tiles = slice(vector_adds(g)[GROUP - 1].stop, GROUP)
                add(nc.gpsimd, rotated, shared, own, all_heads, pool_tiles)
                if g < GROUPS - 2:
                    for o, heads in ((out_0, q_heads), (out_1, k_heads)):
                        store(o, b, t, GROUP, rotated[:, heads])
                else:
                    for first in (0, DUO):
                        for o, heads in ((out_0, q_heads), (out_1, k_heads)):
                            store(o, b, t + first, DUO, rotated[:, heads, first : first + DUO])
            else:
                for o, heads in ((out_0, q_heads), (out_1, k_heads)):
                    add(nc.vector, rotated, shared, own, heads, slice(GROUP - 1, GROUP))
                    store(o, b, t + DUO, DUO, rotated[:, heads, DUO:GROUP])
